import numpy as np
import ml_dtypes


def mxq(x, axis, fmt="e4m3"):
    dtype, down = {"e4m3": (ml_dtypes.float8_e4m3fn, 7), "e5m2": (ml_dtypes.float8_e5m2, 14)}[fmt]
    v = np.moveaxis(np.asarray(x, np.float32).astype(ml_dtypes.bfloat16).astype(np.float64), axis, -1)
    blocks = v.reshape(v.shape[:-1] + (-1, 32))
    amax = np.abs(blocks).max(-1, keepdims=True)
    byte = np.maximum(np.where(amax > 0, np.frexp(amax)[1] - 1 + 127, 0) - down, 1)
    scale = np.exp2(byte - 127.0)
    codes = (blocks / scale).astype(np.float32).astype(dtype).astype(np.float64)
    return np.moveaxis((codes * scale).reshape(v.shape), -1, axis)


WIDE = False


def mx_kscale(k):
    if not WIDE:
        return np.ones(k)
    levels = np.array([10, -10, 5, -5, 0])
    if k % 512:
        return np.exp2(np.random.permutation(np.resize(levels, k // 32))).repeat(32)
    a = np.empty((k // 512, 16))
    for p in range(k // 512):
        a[p, :8] = np.random.permutation(np.resize(levels, 8))
        for g in range(8):
            far = levels[np.abs(levels - a[p, g]) >= 10]
            a[p, g + 8] = far[np.random.randint(len(far))]
    return np.exp2(a.ravel()).repeat(32)


BF16 = ml_dtypes.bfloat16


def bf(x):
    return np.asarray(x, np.float32).astype(BF16)


def f64(x):
    return np.asarray(x).astype(np.float64)


N, L, H, E, HEADS, R = 512, 4, 512, 512, 6, 4
EPS = 1e-12


def l2norm(v):
    n = np.sqrt((v * v).sum(-1, keepdims=True))
    return v / np.maximum(n, EPS)


def setup_inputs():
    s = mx_kscale(H)
    gloss = np.random.standard_normal((N, 1, H))
    amp_w = 0.5 + np.random.random_sample((N, L, 1))
    amp_s = 0.5 + np.random.random_sample((N, 1))
    feature = amp_w * 0.7 * (gloss + np.random.standard_normal((N, L, H)))
    aspect_v = amp_s * np.random.standard_normal((N, H))
    return {"feature": bf(feature * s), "aspect_v": bf(aspect_v * s),
            "W": bf(np.random.standard_normal((HEADS, E, H)) / np.sqrt(H) / s),
            "b": bf(0.2 * np.random.standard_normal((HEADS, E)))}


def reference(feature, aspect_v, W, b):
    wt = mxq(f64(W).transpose(0, 2, 1), 1, "e4m3")
    bias = f64(b)
    q = (mxq(f64(aspect_v), 1, "e4m3") @ wt) + bias[:, None, :]
    fh = (mxq(f64(feature), 2, "e4m3").reshape(N * L, H) @ wt).reshape(HEADS, N, L, E) + bias[:, None, None, :]
    return l2norm(q), l2norm(fh).mean(axis=2)

@@ -1,0 +1,213 @@
+from contextlib import ExitStack
+
+import concourse.mybir as mybir
+from concourse.masks import make_identity
+
+F32 = mybir.dt.float32
+BF16 = mybir.dt.bfloat16
+U32 = mybir.dt.uint32
+U8 = mybir.dt.uint8
+FP8X4 = mybir.dt.float8_e4m3fn_x4
+ALU = mybir.AluOpType
+ACT = mybir.ActivationFunctionType
+
+P = 128
+PACK = 4
+SENSES, WORDS, K = 512, 4, 512
+HEADS, E = 6, 512
+EPS = 1e-12
+
+BLOCKS = 4
+HALVES = 2
+SENSE_BLOCKS = SENSES // P
+GROUPS = HEADS * SENSE_BLOCKS
+TILES = 1 + WORDS
+LAG = 3
+TENSOR_WORDS = 2
+FIRST_PIECES = 3
+TURN_STEP = 1
+FIRST_ADD_STEP = 3
+
+FLOPS = 2 * (SENSES + SENSES * WORDS) * K * HEADS * E
+
+
+def tile_biencodermodel_pa_kernel(tc, feature, aspect_v, W, b, out_0, out_1):
+    nc = tc.nc
+    with ExitStack() as ctx:
+        consts = ctx.enter_context(tc.tile_pool(name="consts", bufs=1))
+        operands = ctx.enter_context(tc.tile_pool(name="operands", bufs=1))
+        staging = ctx.enter_context(tc.tile_pool(name="staging", bufs=FIRST_PIECES))
+        vectors = ctx.enter_context(tc.tile_pool(name="vectors", bufs=(LAG + 1) * TILES))
+        squares = ctx.enter_context(tc.tile_pool(name="squares", bufs=4))
+        norms = ctx.enter_context(tc.tile_pool(name="norms", bufs=LAG + 2))
+        diagonals = ctx.enter_context(tc.tile_pool(name="diagonals", bufs=(LAG + 1) * TENSOR_WORDS))
+        results = ctx.enter_context(tc.tile_pool(name="results", bufs=4))
+        turn_psum = ctx.enter_context(tc.psum_pool(name="turn_psum", bufs=2))
+        sum_psum = ctx.enter_context(tc.psum_pool(name="sum_psum", bufs=2))
+        mx_psum = ctx.enter_context(tc.psum_pool(name="mx_psum", bufs=4))
+        ctx.enter_context(tc.manual_schedule())
+
+        def load_piece(rows, name):
+            raw = operands.tile([P, BLOCKS * K], BF16, name="raw_" + name)
+            nc.sync.dma_start(out=raw[:].rearrange("p (c k) -> p c k", c=BLOCKS), in_=rows)
+            codes = operands.tile([P, BLOCKS * P], U32, name="codes_" + name, align_bytes=64)
+            scales = operands.tile([P, BLOCKS * P], U8, name="scales_" + name, align_bytes=64)
+            return {"raw": raw, "codes": codes, "scales": scales}
+
+        def load_weights(h):
+            return load_piece(W[h].rearrange("(c p) k -> p c k", p=P), "w%d" % h)
+
+        def load_words(i):
+            return load_piece(feature[i * P : (i + 1) * P], "f%d" % i)
+
+        weights = [load_weights(0)]
+        words = [load_words(0)]
+        senses = load_piece(aspect_v.rearrange("(c p) k -> p c k", p=P), "a")
+        bias = consts.tile([P, HEADS * E], BF16)
+        nc.scalar.dma_start(out=bias[:], in_=b.rearrange("h e -> (h e)").partition_broadcast(P))
+        words += [load_words(i) for i in range(1, SENSE_BLOCKS)]
+        weights += [load_weights(h) for h in range(1, HEADS)]
+        pieces = [weights[0], words[0], senses] + words[1:] + weights[1:]
+
+        identity = consts.tile([P, P], F32)
+        make_identity(nc, identity[:])
+        minus_half = consts.tile([P, TILES], F32)
+        nc.gpsimd.memset(minus_half[:], -0.5)
+
+        def turn(piece):
+            row_words = piece["raw"][:].bitcast(F32)
+            grouped = staging.tile([P, BLOCKS * P * PACK], BF16, align_bytes=64)
+            grouped_words = grouped[:].bitcast(F32).rearrange(
+                "p (c r u) -> p c r u", c=BLOCKS, u=HALVES
+            )
+            for pair in range(BLOCKS // 2):
+                turned = turn_psum.tile([P, 2, HALVES, P], F32)
+                for c in range(2):
+                    for u in range(HALVES):
+                        first = (2 * pair + c) * HALVES * P
+                        nc.tensor.transpose(
+                            turned[:, c, u, :],
+                            row_words[:, first + u : first + HALVES * P : HALVES],
+                            identity[:],
+                        )
+                nc.scalar.copy(
+                    out=grouped_words[:, 2 * pair : 2 * pair + 2],
+                    in_=turned[:].rearrange("p c u r -> p c r u"),
+                )
+            return grouped
+
+        def quantise(piece, grouped):
+            nc.vector.quantize_mx(
+                out=piece["codes"][:].bitcast(FP8X4), scales=piece["scales"][:], in_=grouped[:]
+            )
+
+        def project(group, g, t):
+            h, i = divmod(g, SENSE_BLOCKS)
+            rows, block = (senses, i) if t == 0 else (words[i], t - 1)
+            cols = slice(block * P, (block + 1) * P)
+            product = mx_psum.tile([P, E], F32)
+            nc.tensor.matmul_mx(
+                out=product[:],
+                lhsT=rows["codes"][:, cols].bitcast(FP8X4),
+                lhsT_scale=rows["scales"][:, cols],
+                rhs=weights[h]["codes"][:].bitcast(FP8X4),
+                rhs_scale=weights[h]["scales"][:],
+                start=True,
+                stop=True,
+            )
+            vector = vectors.tile([P, E], F32)
+            nc.vector.tensor_tensor(
+                out=vector[:], in0=product[:], in1=bias[:, h * E : (h + 1) * E], op=ALU.add
+            )
+            unread = squares.tile([P, E], F32)
+            nc.scalar.activation(
+                out=unread[:],
+                in_=vector[:],
+                func=ACT.Square,
+                accum_out=group["sum_squares"][:, t : t + 1],
+            )
+            group["vectors"].append(vector)
+
+        def invert_norms(group):
+            clamped = norms.tile([P, TILES], F32)
+            nc.gpsimd.tensor_scalar(
+                out=clamped[:], in0=group["sum_squares"][:], scalar1=EPS * EPS, scalar2=None, op0=ALU.max
+            )
+            inverse = norms.tile([P, TILES], F32)
+            nc.gpsimd.tensor_tensor(out=inverse[:], in0=clamped[:], in1=minus_half[:], op=ALU.pow)
+            mean_weight = norms.tile([P, WORDS], F32)
+            nc.gpsimd.tensor_scalar(
+                out=mean_weight[:], in0=inverse[:, 1:TILES], scalar1=1.0 / WORDS, scalar2=None, op0=ALU.mult
+            )
+            group["inverse"] = inverse
+            group["mean_weight"] = mean_weight
+            group["diagonals"] = []
+            for word in range(WORDS - TENSOR_WORDS, WORDS):
+                diagonal = diagonals.tile([P, P], F32)
+                nc.gpsimd.tensor_scalar(
+                    out=diagonal[:],
+                    in0=identity[:],
+                    scalar1=mean_weight[:, word : word + 1],
+                    scalar2=0.0,
+                    op0=ALU.mult,
+                    op1=ALU.add,
+                )
+                group["diagonals"].append(diagonal)
+
+        def finish(group, g, step):
+            h, i = divmod(g, SENSE_BLOCKS)
+            sense_rows = slice(i * P, (i + 1) * P)
+            if step == 0:
+                last_words = sum_psum.tile([P, E], F32)
+                for n in range(TENSOR_WORDS):
+                    nc.tensor.matmul(
+                        out=last_words[:],
+                        lhsT=group["diagonals"][n][:],
+                        rhs=group["vectors"][1 + WORDS - TENSOR_WORDS + n][:],
+                        start=(n == 0),
+                        stop=(n == TENSOR_WORDS - 1),
+                    )
+                group["mean"] = last_words
+            elif step == 1:
+                unit = results.tile([P, E], F32)
+                nc.scalar.activation(
+                    out=unit[:], in_=group["vectors"][0][:], func=ACT.Copy, scale=group["inverse"][:, 0:1]
+                )
+                nc.sync.dma_start(out=out_0[h, sense_rows, :], in_=unit[:])
+            elif step >= FIRST_ADD_STEP:
+                word = step - FIRST_ADD_STEP
+                mean = results.tile([P, E], F32)
+                nc.vector.scalar_tensor_tensor(
+                    out=mean[:],
+                    in0=group["vectors"][1 + word][:],
+                    scalar=group["mean_weight"][:, word : word + 1],
+                    in1=group["mean"][:],
+                    op0=ALU.mult,
+                    op1=ALU.add,
+                )
+                group["mean"] = mean
+                if word == WORDS - TENSOR_WORDS - 1:
+                    nc.sync.dma_start(out=out_1[h, sense_rows, :], in_=mean[:])
+
+        first_pieces = pieces[:FIRST_PIECES]
+        first_grouped = [turn(piece) for piece in first_pieces]
+        for piece, grouped in zip(first_pieces, first_grouped):
+            quantise(piece, grouped)
+
+        groups = []
+        for g in range(GROUPS + LAG):
+            if g < GROUPS:
+                sum_squares = norms.tile([P, TILES], F32)
+                groups.append({"sum_squares": sum_squares, "vectors": []})
+            piece = pieces[FIRST_PIECES + g] if FIRST_PIECES + g < len(pieces) else None
+            for t in range(TILES):
+                if g >= LAG:
+                    finish(groups[g - LAG], g - LAG, t)
+                if g < GROUPS:
+                    project(groups[g], g, t)
+                if piece is not None and t == TURN_STEP:
+                    grouped = turn(piece)
+            if g < GROUPS:
+                invert_norms(groups[g])
+            if piece is not None:
+                quantise(piece, grouped)

@@ -18,15 +18,14 @@ HEADS, E = 6, 512
 EPS = 1e-12
 
 BLOCKS = 4
-HALVES = 2
+PARITIES = 2
 SENSE_BLOCKS = SENSES // P
+HEAD_PAIR = 2
 GROUPS = HEADS * SENSE_BLOCKS
-TILES = 1 + WORDS
-LAG = 3
+TILES = WORDS + 1
+LAG = 4
 TENSOR_WORDS = 2
-FIRST_PIECES = 3
-TURN_STEP = 1
-FIRST_ADD_STEP = 3
+HALF = BLOCKS // 2
 
 FLOPS = 2 * (SENSES + SENSES * WORDS) * K * HEADS * E
 
@@ -36,23 +35,32 @@ def tile_biencodermodel_pa_kernel(tc, feature, aspect_v, W, b, out_0, out_1):
     with ExitStack() as ctx:
         consts = ctx.enter_context(tc.tile_pool(name="consts", bufs=1))
         operands = ctx.enter_context(tc.tile_pool(name="operands", bufs=1))
-        staging = ctx.enter_context(tc.tile_pool(name="staging", bufs=FIRST_PIECES))
         vectors = ctx.enter_context(tc.tile_pool(name="vectors", bufs=(LAG + 1) * TILES))
         squares = ctx.enter_context(tc.tile_pool(name="squares", bufs=4))
         norms = ctx.enter_context(tc.tile_pool(name="norms", bufs=LAG + 2))
         diagonals = ctx.enter_context(tc.tile_pool(name="diagonals", bufs=(LAG + 1) * TENSOR_WORDS))
-        results = ctx.enter_context(tc.tile_pool(name="results", bufs=4))
+        results = ctx.enter_context(tc.tile_pool(name="results", bufs=3))
         turn_psum = ctx.enter_context(tc.psum_pool(name="turn_psum", bufs=2))
         sum_psum = ctx.enter_context(tc.psum_pool(name="sum_psum", bufs=2))
         mx_psum = ctx.enter_context(tc.psum_pool(name="mx_psum", bufs=4))
         ctx.enter_context(tc.manual_schedule())
 
         def load_piece(rows, name):
-            raw = operands.tile([P, BLOCKS * K], BF16, name="raw_" + name)
-            nc.sync.dma_start(out=raw[:].rearrange("p (c k) -> p c k", c=BLOCKS), in_=rows)
+            raw = []
+            for half in range(2):
+                raw_half = operands.tile([P, HALF * K], BF16, name="raw_%s_%d" % (name, half))
+                nc.sync.dma_start(
+                    out=raw_half[:].rearrange("p (c k) -> p c k", c=HALF),
+                    in_=rows[:, half * HALF : (half + 1) * HALF],
+                )
+                raw.append(raw_half)
             codes = operands.tile([P, BLOCKS * P], U32, name="codes_" + name, align_bytes=64)
             scales = operands.tile([P, BLOCKS * P], U8, name="scales_" + name, align_bytes=64)
-            return {"raw": raw, "codes": codes, "scales": scales}
+            grouped = [
+                operands.tile([P, HALF * P * PACK], BF16, name="grouped_%s_%d" % (name, half), align_bytes=64)
+                for half in range(2)
+            ]
+            return {"raw": raw, "codes": codes, "scales": scales, "grouped": grouped}
 
         def load_weights(h):
             return load_piece(W[h].rearrange("(c p) k -> p c k", p=P), "w%d" % h)
@@ -60,50 +68,62 @@ def tile_biencodermodel_pa_kernel(tc, feature, aspect_v, W, b, out_0, out_1):
         def load_words(i):
             return load_piece(feature[i * P : (i + 1) * P], "f%d" % i)
 
+        bias = []
+
+        def load_bias(queue, h):
+            head_bias = consts.tile([P, E], BF16, name="bias_%d" % h)
+            queue.dma_start(out=head_bias[:], in_=b[h].partition_broadcast(P))
+            bias.append(head_bias)
+
         weights = [load_weights(0)]
+        load_bias(nc.scalar, 0)
         words = [load_words(0)]
         senses = load_piece(aspect_v.rearrange("(c p) k -> p c k", p=P), "a")
-        bias = consts.tile([P, HEADS * E], BF16)
-        nc.scalar.dma_start(out=bias[:], in_=b.rearrange("h e -> (h e)").partition_broadcast(P))
-        words += [load_words(i) for i in range(1, SENSE_BLOCKS)]
-        weights += [load_weights(h) for h in range(1, HEADS)]
-        pieces = [weights[0], words[0], senses] + words[1:] + weights[1:]
+        for h in range(1, HEADS):
+            weights.append(load_weights(h))
+            load_bias(nc.sync, h)
+            if h == HEAD_PAIR - 1:
+                words += [load_words(i) for i in range(1, SENSE_BLOCKS)]
 
         identity = consts.tile([P, P], F32)
         make_identity(nc, identity[:])
-        minus_half = consts.tile([P, TILES], F32)
-        nc.gpsimd.memset(minus_half[:], -0.5)
+        warm = consts.tile([P, 1], F32)
+        nc.vector.memset(warm[:], 1.0)
+        warmed = consts.tile([P, 1], F32)
+        nc.scalar.activation(out=warmed[:], in_=warm[:], func=ACT.Abs_reciprocal_sqrt)
 
-        def turn(piece):
-            row_words = piece["raw"][:].bitcast(F32)
-            grouped = staging.tile([P, BLOCKS * P * PACK], BF16, align_bytes=64)
-            grouped_words = grouped[:].bitcast(F32).rearrange(
-                "p (c r u) -> p c r u", c=BLOCKS, u=HALVES
+        def turn(piece, half):
+            row_words = piece["raw"][half][:].bitcast(F32)
+            turned = turn_psum.tile([P, HALF, PARITIES, P], F32)
+            for c in range(HALF):
+                for u in range(PARITIES):
+                    first = c * PARITIES * P
+                    nc.tensor.transpose(
+                        turned[:, c, u, :],
+                        row_words[:, first + u : first + PARITIES * P : PARITIES],
+                        identity[:],
+                    )
+            piece["turned"] = piece.get("turned", []) + [turned]
+
+        def interleave(piece, half, copy):
+            copy(
+                out=piece["grouped"][half][:].bitcast(F32).rearrange(
+                    "p (c r u) -> p c r u", c=HALF, u=PARITIES
+                ),
+                in_=piece["turned"][half][:].rearrange("p c u r -> p c r u"),
             )
-            for pair in range(BLOCKS // 2):
-                turned = turn_psum.tile([P, 2, HALVES, P], F32)
-                for c in range(2):
-                    for u in range(HALVES):
-                        first = (2 * pair + c) * HALVES * P
-                        nc.tensor.transpose(
-                            turned[:, c, u, :],
-                            row_words[:, first + u : first + HALVES * P : HALVES],
-                            identity[:],
-                        )
-                nc.scalar.copy(
-                    out=grouped_words[:, 2 * pair : 2 * pair + 2],
-                    in_=turned[:].rearrange("p c u r -> p c r u"),
-                )
-            return grouped
 
-        def quantise(piece, grouped):
+        def quantise(piece, half):
+            rows = slice(half * HALF * P, (half + 1) * HALF * P)
             nc.vector.quantize_mx(
-                out=piece["codes"][:].bitcast(FP8X4), scales=piece["scales"][:], in_=grouped[:]
+                out=piece["codes"][:, rows].bitcast(FP8X4),
+                scales=piece["scales"][:, rows],
+                in_=piece["grouped"][half][:],
             )
 
         def project(group, g, t):
-            h, i = divmod(g, SENSE_BLOCKS)
-            rows, block = (senses, i) if t == 0 else (words[i], t - 1)
+            h, i = order[g]
+            rows, block = (words[i], t) if t < WORDS else (senses, i)
             cols = slice(block * P, (block + 1) * P)
             product = mx_psum.tile([P, E], F32)
             nc.tensor.matmul_mx(
@@ -117,97 +137,162 @@ def tile_biencodermodel_pa_kernel(tc, feature, aspect_v, W, b, out_0, out_1):
             )
             vector = vectors.tile([P, E], F32)
             nc.vector.tensor_tensor(
-                out=vector[:], in0=product[:], in1=bias[:, h * E : (h + 1) * E], op=ALU.add
+                out=vector[:], in0=product[:], in1=bias[h][:], op=ALU.add
             )
             unread = squares.tile([P, E], F32)
             nc.scalar.activation(
                 out=unread[:],
                 in_=vector[:],
                 func=ACT.Square,
+                scale=float(WORDS),
                 accum_out=group["sum_squares"][:, t : t + 1],
             )
             group["vectors"].append(vector)
 
-        def invert_norms(group):
+        def weigh_clamp(group):
             clamped = norms.tile([P, TILES], F32)
             nc.gpsimd.tensor_scalar(
-                out=clamped[:], in0=group["sum_squares"][:], scalar1=EPS * EPS, scalar2=None, op0=ALU.max
+                out=clamped[:],
+                in0=group["sum_squares"][:],
+                scalar1=(WORDS * EPS) ** 2,
+                scalar2=None,
+                op0=ALU.max,
             )
-            inverse = norms.tile([P, TILES], F32)
-            nc.gpsimd.tensor_tensor(out=inverse[:], in0=clamped[:], in1=minus_half[:], op=ALU.pow)
-            mean_weight = norms.tile([P, WORDS], F32)
-            nc.gpsimd.tensor_scalar(
-                out=mean_weight[:], in0=inverse[:, 1:TILES], scalar1=1.0 / WORDS, scalar2=None, op0=ALU.mult
+            group["clamped"] = clamped
+
+        def weigh_invert(group):
+            weight = norms.tile([P, TILES], F32)
+            nc.scalar.activation(
+                out=weight[:], in_=group["clamped"][:], func=ACT.Abs_reciprocal_sqrt
             )
-            group["inverse"] = inverse
-            group["mean_weight"] = mean_weight
+            group["weight"] = weight
+
+        def weigh_diagonals(group):
             group["diagonals"] = []
-            for word in range(WORDS - TENSOR_WORDS, WORDS):
+            for t in range(WORDS - TENSOR_WORDS, WORDS):
                 diagonal = diagonals.tile([P, P], F32)
-                nc.gpsimd.tensor_scalar(
+                nc.scalar.activation(
                     out=diagonal[:],
-                    in0=identity[:],
-                    scalar1=mean_weight[:, word : word + 1],
-                    scalar2=0.0,
-                    op0=ALU.mult,
-                    op1=ALU.add,
+                    in_=identity[:],
+                    func=ACT.Copy,
+                    scale=group["weight"][:, t : t + 1],
                 )
                 group["diagonals"].append(diagonal)
 
-        def finish(group, g, step):
-            h, i = divmod(g, SENSE_BLOCKS)
-            sense_rows = slice(i * P, (i + 1) * P)
-            if step == 0:
+        def sum_last_words(group, n):
+            if n == 0:
                 last_words = sum_psum.tile([P, E], F32)
-                for n in range(TENSOR_WORDS):
-                    nc.tensor.matmul(
-                        out=last_words[:],
-                        lhsT=group["diagonals"][n][:],
-                        rhs=group["vectors"][1 + WORDS - TENSOR_WORDS + n][:],
-                        start=(n == 0),
-                        stop=(n == TENSOR_WORDS - 1),
-                    )
-                group["mean"] = last_words
-            elif step == 1:
-                unit = results.tile([P, E], F32)
-                nc.scalar.activation(
-                    out=unit[:], in_=group["vectors"][0][:], func=ACT.Copy, scale=group["inverse"][:, 0:1]
-                )
-                nc.sync.dma_start(out=out_0[h, sense_rows, :], in_=unit[:])
-            elif step >= FIRST_ADD_STEP:
-                word = step - FIRST_ADD_STEP
-                mean = results.tile([P, E], F32)
-                nc.vector.scalar_tensor_tensor(
-                    out=mean[:],
-                    in0=group["vectors"][1 + word][:],
-                    scalar=group["mean_weight"][:, word : word + 1],
-                    in1=group["mean"][:],
-                    op0=ALU.mult,
-                    op1=ALU.add,
-                )
-                group["mean"] = mean
-                if word == WORDS - TENSOR_WORDS - 1:
-                    nc.sync.dma_start(out=out_1[h, sense_rows, :], in_=mean[:])
+                group["last_words"] = last_words
+            nc.tensor.matmul(
+                out=group["last_words"][:],
+                lhsT=group["diagonals"][n][:],
+                rhs=group["vectors"][WORDS - TENSOR_WORDS + n][:],
+                start=(n == 0),
+                stop=(n == TENSOR_WORDS - 1),
+            )
 
-        first_pieces = pieces[:FIRST_PIECES]
-        first_grouped = [turn(piece) for piece in first_pieces]
-        for piece, grouped in zip(first_pieces, first_grouped):
-            quantise(piece, grouped)
+        def weigh_first_word(group):
+            first_word = results.tile([P, E], F32)
+            nc.gpsimd.tensor_scalar(
+                out=first_word[:],
+                in0=group["vectors"][0][:],
+                scalar1=group["weight"][:, 0:1],
+                scalar2=0.0,
+                op0=ALU.mult,
+                op1=ALU.add,
+            )
+            group["first_word"] = first_word
 
+        def finish_senses(group, g):
+            h, i = order[g]
+            unit = results.tile([P, E], F32)
+            nc.gpsimd.tensor_scalar(
+                out=unit[:],
+                in0=group["vectors"][WORDS][:],
+                scalar1=group["weight"][:, WORDS : WORDS + 1],
+                scalar2=float(WORDS),
+                op0=ALU.mult,
+                op1=ALU.mult,
+            )
+            nc.sync.dma_start(out=out_0[h, i * P : (i + 1) * P, :], in_=unit[:])
+
+        def add_second_word(group):
+            later_words = results.tile([P, E], F32)
+            nc.vector.scalar_tensor_tensor(
+                out=later_words[:],
+                in0=group["vectors"][1][:],
+                scalar=group["weight"][:, 1:2],
+                in1=group["last_words"][:],
+                op0=ALU.mult,
+                op1=ALU.add,
+            )
+            group["later_words"] = later_words
+
+        def finish_mean(group, g):
+            h, i = order[g]
+            mean = results.tile([P, E], F32)
+            nc.gpsimd.tensor_tensor(
+                out=mean[:], in0=group["first_word"][:], in1=group["later_words"][:], op=ALU.add
+            )
+            nc.sync.dma_start(out=out_1[h, i * P : (i + 1) * P, :], in_=mean[:])
+
+        for piece in (weights[0], words[0]):
+            turn(piece, 0)
+            turn(piece, 1)
+            interleave(piece, 0, nc.scalar.copy)
+            interleave(piece, 1, nc.vector.tensor_copy)
+            quantise(piece, 0)
+            quantise(piece, 1)
+
+        order = [
+            (h, i)
+            for first in range(0, HEADS, HEAD_PAIR)
+            for i in range(SENSE_BLOCKS)
+            for h in range(first, first + HEAD_PAIR)
+        ]
+        turns = [[(piece, 0), (piece, 1)] for piece in weights[1:HEAD_PAIR] + words[1:] + weights[HEAD_PAIR : 2 * HEAD_PAIR]]
+        turns += [[(piece, half)] for piece in weights[2 * HEAD_PAIR :] for half in range(2)]
+        turns[0] = [(senses, 0), (senses, 1)] + turns[0]
         groups = []
         for g in range(GROUPS + LAG):
             if g < GROUPS:
                 sum_squares = norms.tile([P, TILES], F32)
                 groups.append({"sum_squares": sum_squares, "vectors": []})
-            piece = pieces[FIRST_PIECES + g] if FIRST_PIECES + g < len(pieces) else None
+            turned_halves = turns[g] if g < len(turns) else []
+
+            def back(lag):
+                return groups[g - lag] if lag <= g < GROUPS + lag else None
+
             for t in range(TILES):
-                if g >= LAG:
-                    finish(groups[g - LAG], g - LAG, t)
+                if t == 0 and back(1) is not None:
+                    weigh_clamp(back(1))
+                if t == 1 and back(4) is not None:
+                    add_second_word(back(4))
+                if t == 1 and back(3) is not None:
+                    sum_last_words(back(3), 0)
+                    weigh_first_word(back(3))
+                if t == 1 and back(2) is not None:
+                    finish_senses(back(2), g - 2)
+                if t == 3 and back(3) is not None:
+                    sum_last_words(back(3), 1)
                 if g < GROUPS:
                     project(groups[g], g, t)
-                if piece is not None and t == TURN_STEP:
-                    grouped = turn(piece)
-            if g < GROUPS:
-                invert_norms(groups[g])
-            if piece is not None:
-                quantise(piece, grouped)
+                if t == 1 and back(1) is not None:
+                    weigh_invert(back(1))
+                if t == 3 and back(1) is not None:
+                    weigh_diagonals(back(1))
+                pair = turned_halves[t : t + 2] if t in (0, 2) else []
+                for piece, half in pair:
+                    turn(piece, half)
+                for n, (piece, half) in enumerate(pair):
+                    if n == 0:
+                        interleave(piece, half, nc.scalar.copy)
+                if t in (1, 3):
+                    pair = turned_halves[t - 1 : t + 1]
+                    for n, (piece, half) in enumerate(pair):
+                        if n == 1:
+                            interleave(piece, half, nc.vector.tensor_copy)
+                    for piece, half in pair:
+                        quantise(piece, half)
+            if back(4) is not None:
+                finish_mean(back(4), g - 4)

@@ -166,6 +166,14 @@ def tile_biencodermodel_pa_kernel(tc, feature, aspect_v, W, b, out_0, out_1):
                 out=weight[:], in_=group["clamped"][:], func=ACT.Abs_reciprocal_sqrt
             )
             group["weight"] = weight
+            inverse = norms.tile([P, 1], F32)
+            nc.scalar.activation(
+                out=inverse[:],
+                in_=group["clamped"][:, WORDS : WORDS + 1],
+                func=ACT.Abs_reciprocal_sqrt,
+                scale=1.0 / WORDS**2,
+            )
+            group["inverse"] = inverse
 
         def weigh_diagonals(group):
             group["diagonals"] = []
@@ -209,10 +217,10 @@ def tile_biencodermodel_pa_kernel(tc, feature, aspect_v, W, b, out_0, out_1):
             nc.gpsimd.tensor_scalar(
                 out=unit[:],
                 in0=group["vectors"][WORDS][:],
-                scalar1=group["weight"][:, WORDS : WORDS + 1],
-                scalar2=float(WORDS),
+                scalar1=group["inverse"][:],
+                scalar2=0.0,
                 op0=ALU.mult,
-                op1=ALU.mult,
+                op1=ALU.add,
             )
             nc.sync.dma_start(out=out_0[h, i * P : (i + 1) * P, :], in_=unit[:])
 

@@ -19,13 +19,20 @@ EPS = 1e-12
 
 BLOCKS = 4
 PARITIES = 2
+HALF = BLOCKS // 2
 SENSE_BLOCKS = SENSES // P
 HEAD_PAIR = 2
 GROUPS = HEADS * SENSE_BLOCKS
 TILES = WORDS + 1
-LAG = 4
-TENSOR_WORDS = 2
-HALF = BLOCKS // 2
+TURN_STEPS = (2, 4)
+QUANTISE_STEP = 2
+SENSES_LAG = 2
+SUM_LAG = 3
+MEAN_LAG = 4
+SUM_STEPS = (1, 3)
+ADD_STEP = 4
+LATE_GROUPS = 4
+CLOSING_GROUPS = 1
 
 FLOPS = 2 * (SENSES + SENSES * WORDS) * K * HEADS * E
 
@@ -35,11 +42,13 @@ def tile_biencodermodel_pa_kernel(tc, feature, aspect_v, W, b, out_0, out_1):
     with ExitStack() as ctx:
         consts = ctx.enter_context(tc.tile_pool(name="consts", bufs=1))
         operands = ctx.enter_context(tc.tile_pool(name="operands", bufs=1))
-        vectors = ctx.enter_context(tc.tile_pool(name="vectors", bufs=(LAG + 1) * TILES))
-        squares = ctx.enter_context(tc.tile_pool(name="squares", bufs=4))
-        norms = ctx.enter_context(tc.tile_pool(name="norms", bufs=LAG + 2))
-        diagonals = ctx.enter_context(tc.tile_pool(name="diagonals", bufs=(LAG + 1) * TENSOR_WORDS))
-        results = ctx.enter_context(tc.tile_pool(name="results", bufs=3))
+        staging = ctx.enter_context(tc.tile_pool(name="staging", bufs=4))
+        vectors = ctx.enter_context(tc.tile_pool(name="vectors", bufs=(MEAN_LAG + 1) * TILES))
+        squares = ctx.enter_context(tc.tile_pool(name="squares", bufs=2))
+        norms = ctx.enter_context(tc.tile_pool(name="norms", bufs=MEAN_LAG + 2))
+        halves = ctx.enter_context(tc.tile_pool(name="halves", bufs=16))
+        diagonals = ctx.enter_context(tc.tile_pool(name="diagonals", bufs=2 * MEAN_LAG))
+        results = ctx.enter_context(tc.tile_pool(name="results", bufs=4))
         turn_psum = ctx.enter_context(tc.psum_pool(name="turn_psum", bufs=2))
         sum_psum = ctx.enter_context(tc.psum_pool(name="sum_psum", bufs=2))
         mx_psum = ctx.enter_context(tc.psum_pool(name="mx_psum", bufs=4))
@@ -56,11 +65,7 @@ def tile_biencodermodel_pa_kernel(tc, feature, aspect_v, W, b, out_0, out_1):
                 raw.append(raw_half)
             codes = operands.tile([P, BLOCKS * P], U32, name="codes_" + name, align_bytes=64)
             scales = operands.tile([P, BLOCKS * P], U8, name="scales_" + name, align_bytes=64)
-            grouped = [
-                operands.tile([P, HALF * P * PACK], BF16, name="grouped_%s_%d" % (name, half), align_bytes=64)
-                for half in range(2)
-            ]
-            return {"raw": raw, "codes": codes, "scales": scales, "grouped": grouped}
+            return {"raw": raw, "codes": codes, "scales": scales}
 
         def load_weights(h):
             return load_piece(W[h].rearrange("(c p) k -> p c k", p=P), "w%d" % h)
@@ -87,6 +92,11 @@ def tile_biencodermodel_pa_kernel(tc, feature, aspect_v, W, b, out_0, out_1):
 
         identity = consts.tile([P, P], F32)
         make_identity(nc, identity[:])
+        floor = consts.tile([P, 1], F32)
+        minus_floor = consts.tile([P, 1], F32)
+        small_floor = consts.tile([P, 1], F32)
+        for tile, value in ((floor, WORDS**2), (minus_floor, -(WORDS**2)), (small_floor, 1)):
+            nc.vector.memset(tile[:], value * EPS**2)
         warm = consts.tile([P, 1], F32)
         nc.vector.memset(warm[:], 1.0)
         warmed = consts.tile([P, 1], F32)
@@ -106,19 +116,20 @@ def tile_biencodermodel_pa_kernel(tc, feature, aspect_v, W, b, out_0, out_1):
             piece["turned"] = piece.get("turned", []) + [turned]
 
         def interleave(piece, half, copy):
+            if "grouped" not in piece:
+                grouped = staging.tile([P, BLOCKS * P * PACK], BF16, align_bytes=64)
+                piece["grouped"] = grouped
+            width = HALF * P * PACK
             copy(
-                out=piece["grouped"][half][:].bitcast(F32).rearrange(
-                    "p (c r u) -> p c r u", c=HALF, u=PARITIES
-                ),
+                out=piece["grouped"][:, half * width : (half + 1) * width]
+                .bitcast(F32)
+                .rearrange("p (c r u) -> p c r u", c=HALF, u=PARITIES),
                 in_=piece["turned"][half][:].rearrange("p c u r -> p c r u"),
             )
 
-        def quantise(piece, half):
-            rows = slice(half * HALF * P, (half + 1) * HALF * P)
+        def quantise(piece):
             nc.vector.quantize_mx(
-                out=piece["codes"][:, rows].bitcast(FP8X4),
-                scales=piece["scales"][:, rows],
-                in_=piece["grouped"][half][:],
+                out=piece["codes"][:].bitcast(FP8X4), scales=piece["scales"][:], in_=piece["grouped"][:]
             )
 
         def project(group, g, t):
@@ -149,108 +160,138 @@ def tile_biencodermodel_pa_kernel(tc, feature, aspect_v, W, b, out_0, out_1):
             )
             group["vectors"].append(vector)
 
-        def weigh_clamp(group):
-            clamped = norms.tile([P, TILES], F32)
-            nc.gpsimd.tensor_scalar(
-                out=clamped[:],
-                in0=group["sum_squares"][:],
-                scalar1=(WORDS * EPS) ** 2,
-                scalar2=None,
-                op0=ALU.max,
-            )
-            group["clamped"] = clamped
-
-        def weigh_invert(group):
-            weight = norms.tile([P, TILES], F32)
-            nc.scalar.activation(
-                out=weight[:], in_=group["clamped"][:], func=ACT.Abs_reciprocal_sqrt
-            )
-            group["weight"] = weight
-            inverse = norms.tile([P, 1], F32)
-            nc.scalar.activation(
-                out=inverse[:],
-                in_=group["clamped"][:, WORDS : WORDS + 1],
-                func=ACT.Abs_reciprocal_sqrt,
-                scale=1.0 / WORDS**2,
-            )
-            group["inverse"] = inverse
-
-        def weigh_diagonals(group):
-            group["diagonals"] = []
-            for t in range(WORDS - TENSOR_WORDS, WORDS):
-                diagonal = diagonals.tile([P, P], F32)
+        def weigh(group, step):
+            if step == 0:
+                above = norms.tile([P, TILES], F32)
                 nc.scalar.activation(
-                    out=diagonal[:],
-                    in_=identity[:],
-                    func=ACT.Copy,
-                    scale=group["weight"][:, t : t + 1],
+                    out=above[:], in_=group["sum_squares"][:], func=ACT.Relu, bias=minus_floor[:]
                 )
-                group["diagonals"].append(diagonal)
+                group["above"] = above
+            elif step == 1:
+                weight = norms.tile([P, TILES], F32)
+                nc.scalar.activation(
+                    out=weight[:], in_=group["above"][:], func=ACT.Abs_reciprocal_sqrt, bias=floor[:]
+                )
+                group["weight"] = weight
+            elif step == 2:
+                inverse = norms.tile([P, 1], F32)
+                nc.scalar.activation(
+                    out=inverse[:],
+                    in_=group["above"][:, WORDS : WORDS + 1],
+                    func=ACT.Abs_reciprocal_sqrt,
+                    scale=1.0 / WORDS**2,
+                    bias=small_floor[:],
+                )
+                group["inverse"] = inverse
 
-        def sum_last_words(group, n):
+        def make_diagonal(group, word):
+            diagonal = diagonals.tile([P, P], F32)
+            nc.scalar.activation(
+                out=diagonal[:],
+                in_=identity[:],
+                func=ACT.Copy,
+                scale=group["weight"][:, word : word + 1],
+            )
+            group["diagonals"][word] = diagonal
+
+        def tensor_add(group, n):
             if n == 0:
-                last_words = sum_psum.tile([P, E], F32)
-                group["last_words"] = last_words
+                tensor_sum = sum_psum.tile([P, E], F32)
+                group["sum"] = tensor_sum
+            word = group["tensor"][n]
             nc.tensor.matmul(
-                out=group["last_words"][:],
-                lhsT=group["diagonals"][n][:],
-                rhs=group["vectors"][WORDS - TENSOR_WORDS + n][:],
+                out=group["sum"][:],
+                lhsT=group["diagonals"][word][:],
+                rhs=group["vectors"][word][:],
                 start=(n == 0),
-                stop=(n == TENSOR_WORDS - 1),
+                stop=(n == len(group["tensor"]) - 1),
             )
 
-        def weigh_first_word(group):
-            first_word = results.tile([P, E], F32)
+        def vector_add(group, word):
+            total = results.tile([P, E], F32)
+            nc.vector.scalar_tensor_tensor(
+                out=total[:],
+                in0=group["vectors"][word][:],
+                scalar=group["weight"][:, word : word + 1],
+                in1=group["sum"][:],
+                op0=ALU.mult,
+                op1=ALU.add,
+            )
+            group["sum"] = total
+
+        def vector_sum(group, g, word):
+            h, i = order[g]
+            totals = []
+            for half in range(2):
+                cols = slice(half * E // 2, (half + 1) * E // 2)
+                total = halves.tile([P, E // 2], F32)
+                if word == 0:
+                    nc.vector.tensor_scalar(
+                        out=total[:],
+                        in0=group["vectors"][word][:, cols],
+                        scalar1=group["weight"][:, word : word + 1],
+                        scalar2=None,
+                        op0=ALU.mult,
+                    )
+                else:
+                    nc.vector.scalar_tensor_tensor(
+                        out=total[:],
+                        in0=group["vectors"][word][:, cols],
+                        scalar=group["weight"][:, word : word + 1],
+                        in1=group["sum"][half][:],
+                        op0=ALU.mult,
+                        op1=ALU.add,
+                    )
+                if word == WORDS - 1:
+                    nc.sync.dma_start(out=out_1[h, i * P : (i + 1) * P, cols], in_=total[:])
+                totals.append(total)
+            group["sum"] = totals
+
+        def gpsimd_term(group, word):
+            term = results.tile([P, E], F32)
             nc.gpsimd.tensor_scalar(
-                out=first_word[:],
-                in0=group["vectors"][0][:],
-                scalar1=group["weight"][:, 0:1],
+                out=term[:],
+                in0=group["vectors"][word][:],
+                scalar1=group["weight"][:, word : word + 1],
                 scalar2=0.0,
                 op0=ALU.mult,
                 op1=ALU.add,
             )
-            group["first_word"] = first_word
+            if "term" in group:
+                terms = results.tile([P, E], F32)
+                nc.gpsimd.tensor_tensor(out=terms[:], in0=group["term"][:], in1=term[:], op=ALU.add)
+                group["term"] = terms
+            else:
+                group["term"] = term
+
+        def gpsimd_add(group, g):
+            mean = results.tile([P, E], F32)
+            nc.gpsimd.tensor_tensor(
+                out=mean[:], in0=group["term"][:], in1=group["sum"][:], op=ALU.add
+            )
+            store_mean(group, g, mean)
+
+        def store_mean(group, g, mean):
+            h, i = order[g]
+            nc.sync.dma_start(out=out_1[h, i * P : (i + 1) * P, :], in_=mean[:])
 
         def finish_senses(group, g):
             h, i = order[g]
             unit = results.tile([P, E], F32)
-            nc.gpsimd.tensor_scalar(
-                out=unit[:],
-                in0=group["vectors"][WORDS][:],
-                scalar1=group["inverse"][:],
-                scalar2=0.0,
-                op0=ALU.mult,
-                op1=ALU.add,
-            )
+            if group["late"]:
+                nc.scalar.activation(
+                    out=unit[:], in_=group["vectors"][WORDS][:], func=ACT.Copy, scale=group["inverse"][:]
+                )
+            else:
+                nc.gpsimd.tensor_scalar(
+                    out=unit[:],
+                    in0=group["vectors"][WORDS][:],
+                    scalar1=group["inverse"][:],
+                    scalar2=0.0,
+                    op0=ALU.mult,
+                    op1=ALU.add,
+                )
             nc.sync.dma_start(out=out_0[h, i * P : (i + 1) * P, :], in_=unit[:])
-
-        def add_second_word(group):
-            later_words = results.tile([P, E], F32)
-            nc.vector.scalar_tensor_tensor(
-                out=later_words[:],
-                in0=group["vectors"][1][:],
-                scalar=group["weight"][:, 1:2],
-                in1=group["last_words"][:],
-                op0=ALU.mult,
-                op1=ALU.add,
-            )
-            group["later_words"] = later_words
-
-        def finish_mean(group, g):
-            h, i = order[g]
-            mean = results.tile([P, E], F32)
-            nc.gpsimd.tensor_tensor(
-                out=mean[:], in0=group["first_word"][:], in1=group["later_words"][:], op=ALU.add
-            )
-            nc.sync.dma_start(out=out_1[h, i * P : (i + 1) * P, :], in_=mean[:])
-
-        for piece in (weights[0], words[0]):
-            turn(piece, 0)
-            turn(piece, 1)
-            interleave(piece, 0, nc.scalar.copy)
-            interleave(piece, 1, nc.vector.tensor_copy)
-            quantise(piece, 0)
-            quantise(piece, 1)
 
         order = [
             (h, i)
@@ -258,49 +299,91 @@ def tile_biencodermodel_pa_kernel(tc, feature, aspect_v, W, b, out_0, out_1):
             for i in range(SENSE_BLOCKS)
             for h in range(first, first + HEAD_PAIR)
         ]
-        turns = [[(piece, 0), (piece, 1)] for piece in weights[1:HEAD_PAIR] + words[1:] + weights[HEAD_PAIR : 2 * HEAD_PAIR]]
-        turns += [[(piece, half)] for piece in weights[2 * HEAD_PAIR :] for half in range(2)]
-        turns[0] = [(senses, 0), (senses, 1)] + turns[0]
+
+        def turn_both(piece):
+            turn(piece, 0)
+            turn(piece, 1)
+            interleave(piece, 0, nc.scalar.copy)
+
+        for piece in (weights[0], words[0]):
+            turn_both(piece)
+            interleave(piece, 1, nc.vector.tensor_copy)
+            quantise(piece)
+
+        first_turns = {1: senses, 3: weights[1], 4: words[1]}
+        turns = [[]] + [[(piece, 0), (piece, 1)] for piece in words[2:]]
+        turns += [[(piece, half)] for piece in weights[HEAD_PAIR:] for half in range(2)]
+
         groups = []
-        for g in range(GROUPS + LAG):
+        for g in range(GROUPS + MEAN_LAG):
             if g < GROUPS:
                 sum_squares = norms.tile([P, TILES], F32)
-                groups.append({"sum_squares": sum_squares, "vectors": []})
-            turned_halves = turns[g] if g < len(turns) else []
+                group = {"sum_squares": sum_squares, "vectors": [], "diagonals": {}}
+                group["closing"] = g >= GROUPS - CLOSING_GROUPS
+                group["tensor"] = [3] if g % 3 == 2 else [2, 3]
+                group["late"] = g >= GROUPS - LATE_GROUPS
+                group["gpsimd"] = [] if group["late"] else [0, 2] if g % 3 == 2 else [0]
+                if group["late"]:
+                    group["tensor"] = [2, 3]
+                groups.append(group)
 
-            def back(lag):
-                return groups[g - lag] if lag <= g < GROUPS + lag else None
+            def back(lag, closing):
+                if lag <= g < GROUPS + lag and groups[g - lag]["closing"] == closing:
+                    return groups[g - lag]
+                return None
 
+            turned = turns[g] if g < len(turns) else []
+            ready = [piece for piece, half in turns[g - 1] if half == 1] if 1 <= g <= len(turns) else []
+            if g == 1:
+                ready = [words[1]]
+            last = back(1, False) or back(1, True)
+            summed = back(SUM_LAG, False)
+            sum_steps, add_step = (SUM_STEPS, ADD_STEP) if g < GROUPS else ((1, 1), 1)
             for t in range(TILES):
-                if t == 0 and back(1) is not None:
-                    weigh_clamp(back(1))
-                if t == 1 and back(4) is not None:
-                    add_second_word(back(4))
-                if t == 1 and back(3) is not None:
-                    sum_last_words(back(3), 0)
-                    weigh_first_word(back(3))
-                if t == 1 and back(2) is not None:
-                    finish_senses(back(2), g - 2)
-                if t == 3 and back(3) is not None:
-                    sum_last_words(back(3), 1)
+                if t in TURN_STEPS[: len(turned)]:
+                    turn(*turned[TURN_STEPS.index(t)])
+                if t == 1 and summed is not None:
+                    for word in summed["gpsimd"]:
+                        gpsimd_term(summed, word)
+                if t == 1 and back(SENSES_LAG, False) is not None:
+                    finish_senses(back(SENSES_LAG, False), g - SENSES_LAG)
+                if summed is not None:
+                    for n in range(len(summed["tensor"])):
+                        if sum_steps[n] == t:
+                            tensor_add(summed, n)
+                    if t == add_step:
+                        vector_add(summed, 1)
+                        if not summed["gpsimd"]:
+                            vector_add(summed, 0)
+                            store_mean(summed, g - SUM_LAG, summed["sum"])
                 if g < GROUPS:
                     project(groups[g], g, t)
-                if t == 1 and back(1) is not None:
-                    weigh_invert(back(1))
-                if t == 3 and back(1) is not None:
-                    weigh_diagonals(back(1))
-                pair = turned_halves[t : t + 2] if t in (0, 2) else []
-                for piece, half in pair:
-                    turn(piece, half)
-                for n, (piece, half) in enumerate(pair):
-                    if n == 0:
-                        interleave(piece, half, nc.scalar.copy)
-                if t in (1, 3):
-                    pair = turned_halves[t - 1 : t + 1]
-                    for n, (piece, half) in enumerate(pair):
-                        if n == 1:
-                            interleave(piece, half, nc.vector.tensor_copy)
-                    for piece, half in pair:
-                        quantise(piece, half)
-            if back(4) is not None:
-                finish_mean(back(4), g - 4)
+                if last is not None:
+                    weigh(last, t)
+                    if t == 3 and not last["closing"]:
+                        for word in last["tensor"]:
+                            make_diagonal(last, word)
+                    if t >= 1 and last["closing"]:
+                        vector_sum(last, g - 1, t - 1)
+                    if t == 3 and last["closing"]:
+                        finish_senses(last, g - 1)
+                if t in TURN_STEPS[: len(turned)]:
+                    n = TURN_STEPS.index(t)
+                    interleave(*turned[n], nc.scalar.copy if n == 0 else nc.vector.tensor_copy)
+                if t == QUANTISE_STEP:
+                    for piece in ready:
+                        quantise(piece)
+                if g == 0:
+                    if t == 2:
+                        interleave(senses, 1, nc.vector.tensor_copy)
+                    if t == 3:
+                        quantise(senses)
+                    if t == 4:
+                        interleave(weights[1], 1, nc.vector.tensor_copy)
+                        quantise(weights[1])
+                    if t in first_turns:
+                        turn_both(first_turns[t])
+                    if t == 4:
+                        interleave(words[1], 1, nc.vector.tensor_copy)
+            if back(MEAN_LAG, False) is not None and back(MEAN_LAG, False)["gpsimd"]:
+                gpsimd_add(back(MEAN_LAG, False), g - MEAN_LAG)

@@ -31,8 +31,7 @@ SUM_LAG = 3
 MEAN_LAG = 4
 SUM_STEPS = (1, 3)
 ADD_STEP = 4
-LATE_GROUPS = 4
-CLOSING_GROUPS = 1
+LATE_GROUPS = 3
 
 FLOPS = 2 * (SENSES + SENSES * WORDS) * K * HEADS * E
 
@@ -46,9 +45,10 @@ def tile_biencodermodel_pa_kernel(tc, feature, aspect_v, W, b, out_0, out_1):
         vectors = ctx.enter_context(tc.tile_pool(name="vectors", bufs=(MEAN_LAG + 1) * TILES))
         squares = ctx.enter_context(tc.tile_pool(name="squares", bufs=2))
         norms = ctx.enter_context(tc.tile_pool(name="norms", bufs=MEAN_LAG + 2))
-        halves = ctx.enter_context(tc.tile_pool(name="halves", bufs=16))
+        column_halves = ctx.enter_context(tc.tile_pool(name="column_halves", bufs=4 * WORDS))
         diagonals = ctx.enter_context(tc.tile_pool(name="diagonals", bufs=2 * MEAN_LAG))
-        results = ctx.enter_context(tc.tile_pool(name="results", bufs=4))
+        sums = ctx.enter_context(tc.tile_pool(name="sums", bufs=4))
+        results = ctx.enter_context(tc.tile_pool(name="results", bufs=3))
         turn_psum = ctx.enter_context(tc.psum_pool(name="turn_psum", bufs=2))
         sum_psum = ctx.enter_context(tc.psum_pool(name="sum_psum", bufs=2))
         mx_psum = ctx.enter_context(tc.psum_pool(name="mx_psum", bufs=4))
@@ -92,11 +92,22 @@ def tile_biencodermodel_pa_kernel(tc, feature, aspect_v, W, b, out_0, out_1):
 
         identity = consts.tile([P, P], F32)
         make_identity(nc, identity[:])
+        scaled_bias = []
+        for h in range(HEADS):
+            scaled = consts.tile([P, E], BF16, name="scaled_bias_%d" % h)
+            nc.gpsimd.tensor_scalar(
+                out=scaled[:],
+                in0=bias[h][:],
+                scalar1=float(WORDS),
+                scalar2=0.0,
+                op0=ALU.mult,
+                op1=ALU.add,
+            )
+            scaled_bias.append(scaled)
         floor = consts.tile([P, 1], F32)
+        nc.vector.memset(floor[:], (WORDS * EPS) ** 2)
         minus_floor = consts.tile([P, 1], F32)
-        small_floor = consts.tile([P, 1], F32)
-        for tile, value in ((floor, WORDS**2), (minus_floor, -(WORDS**2)), (small_floor, 1)):
-            nc.vector.memset(tile[:], value * EPS**2)
+        nc.vector.memset(minus_floor[:], -((WORDS * EPS) ** 2))
         warm = consts.tile([P, 1], F32)
         nc.vector.memset(warm[:], 1.0)
         warmed = consts.tile([P, 1], F32)
@@ -127,9 +138,12 @@ def tile_biencodermodel_pa_kernel(tc, feature, aspect_v, W, b, out_0, out_1):
                 in_=piece["turned"][half][:].rearrange("p c u r -> p c r u"),
             )
 
-        def quantise(piece):
+        def quantise(piece, first_half=0, halves=2):
+            first, last = first_half * HALF * P, (first_half + halves) * HALF * P
             nc.vector.quantize_mx(
-                out=piece["codes"][:].bitcast(FP8X4), scales=piece["scales"][:], in_=piece["grouped"][:]
+                out=piece["codes"][:, first:last].bitcast(FP8X4),
+                scales=piece["scales"][:, first:last],
+                in_=piece["grouped"][:, first * PACK : last * PACK],
             )
 
         def project(group, g, t):
@@ -147,18 +161,28 @@ def tile_biencodermodel_pa_kernel(tc, feature, aspect_v, W, b, out_0, out_1):
                 stop=True,
             )
             vector = vectors.tile([P, E], F32)
-            nc.vector.tensor_tensor(
-                out=vector[:], in0=product[:], in1=bias[h][:], op=ALU.add
-            )
+            if t < WORDS:
+                nc.vector.tensor_tensor(
+                    out=vector[:], in0=product[:], in1=bias[h][:], op=ALU.add
+                )
+            else:
+                nc.vector.scalar_tensor_tensor(
+                    out=vector[:],
+                    in0=product[:],
+                    scalar=float(WORDS),
+                    in1=scaled_bias[h][:],
+                    op0=ALU.mult,
+                    op1=ALU.add,
+                )
             unread = squares.tile([P, E], F32)
             nc.scalar.activation(
                 out=unread[:],
                 in_=vector[:],
                 func=ACT.Square,
-                scale=float(WORDS),
+                scale=float(WORDS) if t < WORDS else 1.0,
                 accum_out=group["sum_squares"][:, t : t + 1],
             )
-            group["vectors"].append(vector)
+            group["vectors"][t] = vector
 
         def weigh(group, step):
             if step == 0:
@@ -167,22 +191,12 @@ def tile_biencodermodel_pa_kernel(tc, feature, aspect_v, W, b, out_0, out_1):
                     out=above[:], in_=group["sum_squares"][:], func=ACT.Relu, bias=minus_floor[:]
                 )
                 group["above"] = above
-            elif step == 1:
+            else:
                 weight = norms.tile([P, TILES], F32)
                 nc.scalar.activation(
                     out=weight[:], in_=group["above"][:], func=ACT.Abs_reciprocal_sqrt, bias=floor[:]
                 )
                 group["weight"] = weight
-            elif step == 2:
-                inverse = norms.tile([P, 1], F32)
-                nc.scalar.activation(
-                    out=inverse[:],
-                    in_=group["above"][:, WORDS : WORDS + 1],
-                    func=ACT.Abs_reciprocal_sqrt,
-                    scale=1.0 / WORDS**2,
-                    bias=small_floor[:],
-                )
-                group["inverse"] = inverse
 
         def make_diagonal(group, word):
             diagonal = diagonals.tile([P, P], F32)
@@ -208,7 +222,7 @@ def tile_biencodermodel_pa_kernel(tc, feature, aspect_v, W, b, out_0, out_1):
             )
 
         def vector_add(group, word):
-            total = results.tile([P, E], F32)
+            total = sums.tile([P, E], F32)
             nc.vector.scalar_tensor_tensor(
                 out=total[:],
                 in0=group["vectors"][word][:],
@@ -219,17 +233,31 @@ def tile_biencodermodel_pa_kernel(tc, feature, aspect_v, W, b, out_0, out_1):
             )
             group["sum"] = total
 
+        def weigh_alone(group, t, step):
+            if step == 0:
+                above = norms.tile([P, 1], F32, name="above_alone")
+                nc.scalar.activation(
+                    out=above[:], in_=group["sum_squares"][:, t : t + 1], func=ACT.Relu, bias=minus_floor[:]
+                )
+                group["above"][t] = above
+            else:
+                weight = norms.tile([P, 1], F32, name="weight_alone")
+                nc.scalar.activation(
+                    out=weight[:], in_=group["above"][t][:], func=ACT.Abs_reciprocal_sqrt, bias=floor[:]
+                )
+                group["weights"][t] = weight
+
         def vector_sum(group, g, word):
             h, i = order[g]
             totals = []
             for half in range(2):
                 cols = slice(half * E // 2, (half + 1) * E // 2)
-                total = halves.tile([P, E // 2], F32)
+                total = column_halves.tile([P, E // 2], F32)
                 if word == 0:
                     nc.vector.tensor_scalar(
                         out=total[:],
                         in0=group["vectors"][word][:, cols],
-                        scalar1=group["weight"][:, word : word + 1],
+                        scalar1=group["weights"][word][:],
                         scalar2=None,
                         op0=ALU.mult,
                     )
@@ -237,15 +265,15 @@ def tile_biencodermodel_pa_kernel(tc, feature, aspect_v, W, b, out_0, out_1):
                     nc.vector.scalar_tensor_tensor(
                         out=total[:],
                         in0=group["vectors"][word][:, cols],
-                        scalar=group["weight"][:, word : word + 1],
-                        in1=group["sum"][half][:],
+                        scalar=group["weights"][word][:],
+                        in1=group["totals"][half][:],
                         op0=ALU.mult,
                         op1=ALU.add,
                     )
                 if word == WORDS - 1:
                     nc.sync.dma_start(out=out_1[h, i * P : (i + 1) * P, cols], in_=total[:])
                 totals.append(total)
-            group["sum"] = totals
+            group["totals"] = totals
 
         def gpsimd_term(group, word):
             term = results.tile([P, E], F32)
@@ -278,15 +306,15 @@ def tile_biencodermodel_pa_kernel(tc, feature, aspect_v, W, b, out_0, out_1):
         def finish_senses(group, g):
             h, i = order[g]
             unit = results.tile([P, E], F32)
-            if group["late"]:
+            if g == GROUPS - 1:
                 nc.scalar.activation(
-                    out=unit[:], in_=group["vectors"][WORDS][:], func=ACT.Copy, scale=group["inverse"][:]
+                    out=unit[:], in_=group["vectors"][WORDS][:], func=ACT.Copy, scale=group["weights"][WORDS][:]
                 )
             else:
                 nc.gpsimd.tensor_scalar(
                     out=unit[:],
                     in0=group["vectors"][WORDS][:],
-                    scalar1=group["inverse"][:],
+                    scalar1=group["weight"][:, WORDS : WORDS + 1],
                     scalar2=0.0,
                     op0=ALU.mult,
                     op1=ALU.add,
@@ -300,17 +328,24 @@ def tile_biencodermodel_pa_kernel(tc, feature, aspect_v, W, b, out_0, out_1):
             for h in range(first, first + HEAD_PAIR)
         ]
 
-        def turn_both(piece):
-            turn(piece, 0)
-            turn(piece, 1)
-            interleave(piece, 0, nc.scalar.copy)
+        def split(g):
+            if g >= GROUPS - LATE_GROUPS:
+                return {"tensor": [2, 3], "vector": [1, 0], "gpsimd": []}
+            if g % 3 == 2:
+                return {"tensor": [3], "vector": [1], "gpsimd": [0, 2]}
+            return {"tensor": [2, 3], "vector": [1], "gpsimd": [0]}
 
-        for piece in (weights[0], words[0]):
-            turn_both(piece)
-            interleave(piece, 1, nc.vector.tensor_copy)
-            quantise(piece)
+        turn(weights[0], 0)
+        turn(weights[0], 1)
+        interleave(weights[0], 0, nc.scalar.copy)
+        interleave(weights[0], 1, nc.vector.tensor_copy)
+        quantise(weights[0])
+        turn(words[0], 0)
+        turn(words[0], 1)
+        interleave(words[0], 0, nc.scalar.copy)
+        interleave(words[0], 1, nc.scalar.copy)
+        quantise(words[0], 0, 1)
 
-        first_turns = {1: senses, 3: weights[1], 4: words[1]}
         turns = [[]] + [[(piece, 0), (piece, 1)] for piece in words[2:]]
         turns += [[(piece, half)] for piece in weights[HEAD_PAIR:] for half in range(2)]
 
@@ -318,55 +353,61 @@ def tile_biencodermodel_pa_kernel(tc, feature, aspect_v, W, b, out_0, out_1):
         for g in range(GROUPS + MEAN_LAG):
             if g < GROUPS:
                 sum_squares = norms.tile([P, TILES], F32)
-                group = {"sum_squares": sum_squares, "vectors": [], "diagonals": {}}
-                group["closing"] = g >= GROUPS - CLOSING_GROUPS
-                group["tensor"] = [3] if g % 3 == 2 else [2, 3]
-                group["late"] = g >= GROUPS - LATE_GROUPS
-                group["gpsimd"] = [] if group["late"] else [0, 2] if g % 3 == 2 else [0]
-                if group["late"]:
-                    group["tensor"] = [2, 3]
+                group = {"sum_squares": sum_squares, "vectors": {}, "weights": {}, "above": {}, "diagonals": {}}
+                group.update(split(g))
                 groups.append(group)
+            closing = g == GROUPS - 1
 
-            def back(lag, closing):
-                if lag <= g < GROUPS + lag and groups[g - lag]["closing"] == closing:
-                    return groups[g - lag]
-                return None
+            def back(lag):
+                return groups[g - lag] if lag <= g < GROUPS - 1 + lag else None
 
             turned = turns[g] if g < len(turns) else []
             ready = [piece for piece, half in turns[g - 1] if half == 1] if 1 <= g <= len(turns) else []
             if g == 1:
                 ready = [words[1]]
-            last = back(1, False) or back(1, True)
-            summed = back(SUM_LAG, False)
-            sum_steps, add_step = (SUM_STEPS, ADD_STEP) if g < GROUPS else ((1, 1), 1)
             for t in range(TILES):
                 if t in TURN_STEPS[: len(turned)]:
                     turn(*turned[TURN_STEPS.index(t)])
-                if t == 1 and summed is not None:
-                    for word in summed["gpsimd"]:
-                        gpsimd_term(summed, word)
-                if t == 1 and back(SENSES_LAG, False) is not None:
-                    finish_senses(back(SENSES_LAG, False), g - SENSES_LAG)
-                if summed is not None:
-                    for n in range(len(summed["tensor"])):
-                        if sum_steps[n] == t:
-                            tensor_add(summed, n)
-                    if t == add_step:
-                        vector_add(summed, 1)
-                        if not summed["gpsimd"]:
-                            vector_add(summed, 0)
-                            store_mean(summed, g - SUM_LAG, summed["sum"])
+                if t == 1 and back(SUM_LAG) is not None:
+                    for word in back(SUM_LAG)["gpsimd"]:
+                        gpsimd_term(back(SUM_LAG), word)
+                if t == 2 and back(SENSES_LAG) is not None:
+                    finish_senses(back(SENSES_LAG), g - SENSES_LAG)
+                for lag in (SUM_LAG, SUM_LAG - 1):
+                    f = g - lag
+                    if back(lag) is None or (f >= GROUPS - LATE_GROUPS) != (lag < SUM_LAG):
+                        continue
+                    steps = SUM_STEPS if lag == SUM_LAG else (TILES - 1, TILES - 1)
+                    for n in range(len(back(lag)["tensor"])):
+                        if t == steps[n]:
+                            tensor_add(back(lag), n)
+                f = g - SUM_LAG
+                if t == ADD_STEP and 0 <= f < GROUPS - LATE_GROUPS:
+                    vector_add(groups[f], 1)
+                if t == 0 and g - SUM_LAG >= GROUPS - LATE_GROUPS and back(SUM_LAG) is not None:
+                    for word in back(SUM_LAG)["vector"]:
+                        vector_add(back(SUM_LAG), word)
+                    if not back(SUM_LAG)["gpsimd"]:
+                        store_mean(back(SUM_LAG), g - SUM_LAG, back(SUM_LAG)["sum"])
+                if g == GROUPS and t == 1:
+                    finish_senses(group, g - 1)
+                    for word in range(2, WORDS):
+                        vector_sum(group, g - 1, word)
                 if g < GROUPS:
-                    project(groups[g], g, t)
-                if last is not None:
-                    weigh(last, t)
-                    if t == 3 and not last["closing"]:
-                        for word in last["tensor"]:
-                            make_diagonal(last, word)
-                    if t >= 1 and last["closing"]:
-                        vector_sum(last, g - 1, t - 1)
-                    if t == 3 and last["closing"]:
-                        finish_senses(last, g - 1)
+                    project(groups[g], g, (t - 1) % TILES if closing else t)
+                if back(1) is not None:
+                    if t < 2:
+                        weigh(back(1), t)
+                    if t == 3:
+                        for word in back(1)["tensor"]:
+                            make_diagonal(back(1), word)
+                if closing and t >= 1:
+                    weigh_alone(group, (t - 2) % TILES, 0)
+                if closing and t >= 2:
+                    weigh_alone(group, (t - 3) % TILES, 1)
+                if closing and t == 4:
+                    vector_sum(group, g, 0)
+                    vector_sum(group, g, 1)
                 if t in TURN_STEPS[: len(turned)]:
                     n = TURN_STEPS.index(t)
                     interleave(*turned[n], nc.scalar.copy if n == 0 else nc.vector.tensor_copy)
@@ -374,6 +415,8 @@ def tile_biencodermodel_pa_kernel(tc, feature, aspect_v, W, b, out_0, out_1):
                     for piece in ready:
                         quantise(piece)
                 if g == 0:
+                    if t == 1:
+                        quantise(words[0], 1, 1)
                     if t == 2:
                         interleave(senses, 1, nc.vector.tensor_copy)
                     if t == 3:
@@ -381,9 +424,16 @@ def tile_biencodermodel_pa_kernel(tc, feature, aspect_v, W, b, out_0, out_1):
                     if t == 4:
                         interleave(weights[1], 1, nc.vector.tensor_copy)
                         quantise(weights[1])
-                    if t in first_turns:
-                        turn_both(first_turns[t])
+                    for step, piece in ((1, senses), (3, weights[1]), (4, words[1])):
+                        if t == step:
+                            turn(piece, 0)
+                            turn(piece, 1)
+                            interleave(piece, 0, nc.scalar.copy)
                     if t == 4:
                         interleave(words[1], 1, nc.vector.tensor_copy)
-            if back(MEAN_LAG, False) is not None and back(MEAN_LAG, False)["gpsimd"]:
-                gpsimd_add(back(MEAN_LAG, False), g - MEAN_LAG)
+            if closing:
+                weigh_alone(group, WORDS - 1, 0)
+                weigh_alone(group, WORDS - 2, 1)
+                weigh_alone(group, WORDS - 1, 1)
+            if back(MEAN_LAG) is not None and back(MEAN_LAG)["gpsimd"]:
+                gpsimd_add(back(MEAN_LAG), g - MEAN_LAG)

@@ -29,7 +29,7 @@ QUANTISE_STEP = 2
 SENSES_LAG = 2
 SUM_LAG = 3
 MEAN_LAG = 4
-SUM_STEPS = (1, 3)
+SUM_STEPS = (1, 1)
 ADD_STEP = 4
 LATE_GROUPS = 3
 
@@ -47,11 +47,10 @@ def tile_biencodermodel_pa_kernel(tc, feature, aspect_v, W, b, out_0, out_1):
         norms = ctx.enter_context(tc.tile_pool(name="norms", bufs=MEAN_LAG + 2))
         column_halves = ctx.enter_context(tc.tile_pool(name="column_halves", bufs=4 * WORDS))
         diagonals = ctx.enter_context(tc.tile_pool(name="diagonals", bufs=2 * MEAN_LAG))
-        sums = ctx.enter_context(tc.tile_pool(name="sums", bufs=4))
+        sums = ctx.enter_context(tc.tile_pool(name="sums", bufs=8))
         results = ctx.enter_context(tc.tile_pool(name="results", bufs=3))
-        turn_psum = ctx.enter_context(tc.psum_pool(name="turn_psum", bufs=2))
         sum_psum = ctx.enter_context(tc.psum_pool(name="sum_psum", bufs=2))
-        mx_psum = ctx.enter_context(tc.psum_pool(name="mx_psum", bufs=4))
+        main_psum = ctx.enter_context(tc.psum_pool(name="main_psum", bufs=6))
         ctx.enter_context(tc.manual_schedule())
 
         def load_piece(rows, name):
@@ -81,8 +80,8 @@ def tile_biencodermodel_pa_kernel(tc, feature, aspect_v, W, b, out_0, out_1):
             bias.append(head_bias)
 
         weights = [load_weights(0)]
-        load_bias(nc.scalar, 0)
         words = [load_words(0)]
+        load_bias(nc.sync, 0)
         senses = load_piece(aspect_v.rearrange("(c p) k -> p c k", p=P), "a")
         for h in range(1, HEADS):
             weights.append(load_weights(h))
@@ -115,7 +114,7 @@ def tile_biencodermodel_pa_kernel(tc, feature, aspect_v, W, b, out_0, out_1):
 
         def turn(piece, half):
             row_words = piece["raw"][half][:].bitcast(F32)
-            turned = turn_psum.tile([P, HALF, PARITIES, P], F32)
+            turned = main_psum.tile([P, HALF, PARITIES, P], F32, name="bank")
             for c in range(HALF):
                 for u in range(PARITIES):
                     first = c * PARITIES * P
@@ -150,7 +149,7 @@ def tile_biencodermodel_pa_kernel(tc, feature, aspect_v, W, b, out_0, out_1):
             h, i = order[g]
             rows, block = (words[i], t) if t < WORDS else (senses, i)
             cols = slice(block * P, (block + 1) * P)
-            product = mx_psum.tile([P, E], F32)
+            product = main_psum.tile([P, E], F32, name="bank")
             nc.tensor.matmul_mx(
                 out=product[:],
                 lhsT=rows["codes"][:, cols].bitcast(FP8X4),
@@ -331,7 +330,7 @@ def tile_biencodermodel_pa_kernel(tc, feature, aspect_v, W, b, out_0, out_1):
         def split(g):
             if g >= GROUPS - LATE_GROUPS:
                 return {"tensor": [2, 3], "vector": [1, 0], "gpsimd": []}
-            if g % 3 == 2:
+            if g % 3 == 0:
                 return {"tensor": [3], "vector": [1], "gpsimd": [0, 2]}
             return {"tensor": [2, 3], "vector": [1], "gpsimd": [0]}
 
@@ -345,6 +344,7 @@ def tile_biencodermodel_pa_kernel(tc, feature, aspect_v, W, b, out_0, out_1):
         interleave(words[0], 0, nc.scalar.copy)
         interleave(words[0], 1, nc.scalar.copy)
         quantise(words[0], 0, 1)
+        quantise(words[0], 1, 1)
 
         turns = [[]] + [[(piece, 0), (piece, 1)] for piece in words[2:]]
         turns += [[(piece, half)] for piece in weights[HEAD_PAIR:] for half in range(2)]
@@ -391,7 +391,7 @@ def tile_biencodermodel_pa_kernel(tc, feature, aspect_v, W, b, out_0, out_1):
                         store_mean(back(SUM_LAG), g - SUM_LAG, back(SUM_LAG)["sum"])
                 if g == GROUPS and t == 1:
                     finish_senses(group, g - 1)
-                    for word in range(2, WORDS):
+                    for word in range(1, WORDS):
                         vector_sum(group, g - 1, word)
                 if g < GROUPS:
                     project(groups[g], g, (t - 1) % TILES if closing else t)
@@ -407,7 +407,6 @@ def tile_biencodermodel_pa_kernel(tc, feature, aspect_v, W, b, out_0, out_1):
                     weigh_alone(group, (t - 3) % TILES, 1)
                 if closing and t == 4:
                     vector_sum(group, g, 0)
-                    vector_sum(group, g, 1)
                 if t in TURN_STEPS[: len(turned)]:
                     n = TURN_STEPS.index(t)
                     interleave(*turned[n], nc.scalar.copy if n == 0 else nc.vector.tensor_copy)
@@ -416,21 +415,22 @@ def tile_biencodermodel_pa_kernel(tc, feature, aspect_v, W, b, out_0, out_1):
                         quantise(piece)
                 if g == 0:
                     if t == 1:
-                        quantise(words[0], 1, 1)
-                    if t == 2:
-                        interleave(senses, 1, nc.vector.tensor_copy)
+                        turn(senses, 0)
+                        turn(senses, 1)
+                        interleave(senses, 0, nc.scalar.copy)
+                        interleave(senses, 1, nc.scalar.copy)
                     if t == 3:
                         quantise(senses)
+                        turn(weights[1], 0)
+                        turn(weights[1], 1)
+                        interleave(weights[1], 0, nc.scalar.copy)
+                        interleave(weights[1], 1, nc.scalar.copy)
                     if t == 4:
-                        interleave(weights[1], 1, nc.vector.tensor_copy)
                         quantise(weights[1])
-                    for step, piece in ((1, senses), (3, weights[1]), (4, words[1])):
-                        if t == step:
-                            turn(piece, 0)
-                            turn(piece, 1)
-                            interleave(piece, 0, nc.scalar.copy)
-                    if t == 4:
-                        interleave(words[1], 1, nc.vector.tensor_copy)
+                        turn(words[1], 0)
+                        turn(words[1], 1)
+                        interleave(words[1], 0, nc.scalar.copy)
+                        interleave(words[1], 1, nc.scalar.copy)
             if closing:
                 weigh_alone(group, WORDS - 1, 0)
                 weigh_alone(group, WORDS - 2, 1)

@@ -29,9 +29,12 @@ QUANTISE_STEP = 2
 SENSES_LAG = 2
 SUM_LAG = 3
 MEAN_LAG = 4
-SUM_STEPS = (1, 1)
+SUM_STEP = 1
+SENSES_STEP = 2
 ADD_STEP = 4
+BIAS_LEAD = 6
 LATE_GROUPS = 3
+EASED_GROUPS = 6
 
 FLOPS = 2 * (SENSES + SENSES * WORDS) * K * HEADS * E
 
@@ -72,37 +75,30 @@ def tile_biencodermodel_pa_kernel(tc, feature, aspect_v, W, b, out_0, out_1):
         def load_words(i):
             return load_piece(feature[i * P : (i + 1) * P], "f%d" % i)
 
-        bias = []
-
-        def load_bias(queue, h):
-            head_bias = consts.tile([P, E], BF16, name="bias_%d" % h)
-            queue.dma_start(out=head_bias[:], in_=b[h].partition_broadcast(P))
-            bias.append(head_bias)
+        loaded_row = consts.tile([P, HEAD_PAIR * E], BF16)
+        nc.sync.dma_start(
+            out=loaded_row[0:1, :], in_=b[0:HEAD_PAIR].rearrange("(o h) e -> o (h e)", o=1)
+        )
+        bias_row = consts.tile([P, HEAD_PAIR * E], BF16)
+        nc.vector.memset(bias_row[:].bitcast(F32), 0.0)
+        ones = consts.tile([P, P], BF16)
+        nc.vector.memset(ones[:], 1.0)
 
         weights = [load_weights(0)]
         words = [load_words(0)]
-        load_bias(nc.sync, 0)
         senses = load_piece(aspect_v.rearrange("(c p) k -> p c k", p=P), "a")
-        for h in range(1, HEADS):
-            weights.append(load_weights(h))
-            load_bias(nc.sync, h)
-            if h == HEAD_PAIR - 1:
-                words += [load_words(i) for i in range(1, SENSE_BLOCKS)]
+        weights.append(load_weights(1))
+        words += [load_words(i) for i in range(1, SENSE_BLOCKS)]
+        weights += [load_weights(h) for h in range(HEAD_PAIR, HEADS)]
+        first_biases = consts.tile([P, HEAD_PAIR * E], BF16)
+        bias = [first_biases[:, h * E : (h + 1) * E] for h in range(HEAD_PAIR)]
+        for h in range(HEAD_PAIR, HEADS):
+            head_bias = consts.tile([P, E], BF16, name="bias_%d" % h)
+            nc.sync.dma_start(out=head_bias[:], in_=b[h].partition_broadcast(P))
+            bias.append(head_bias[:])
 
         identity = consts.tile([P, P], F32)
         make_identity(nc, identity[:])
-        scaled_bias = []
-        for h in range(HEADS):
-            scaled = consts.tile([P, E], BF16, name="scaled_bias_%d" % h)
-            nc.gpsimd.tensor_scalar(
-                out=scaled[:],
-                in0=bias[h][:],
-                scalar1=float(WORDS),
-                scalar2=0.0,
-                op0=ALU.mult,
-                op1=ALU.add,
-            )
-            scaled_bias.append(scaled)
         floor = consts.tile([P, 1], F32)
         nc.vector.memset(floor[:], (WORDS * EPS) ** 2)
         minus_floor = consts.tile([P, 1], F32)
@@ -111,6 +107,34 @@ def tile_biencodermodel_pa_kernel(tc, feature, aspect_v, W, b, out_0, out_1):
         nc.vector.memset(warm[:], 1.0)
         warmed = consts.tile([P, 1], F32)
         nc.scalar.activation(out=warmed[:], in_=warm[:], func=ACT.Abs_reciprocal_sqrt)
+
+        nc.vector.tensor_copy(out=bias_row[0:1, :], in_=loaded_row[0:1, :])
+
+        def spread_biases():
+            spread = sum_psum.tile([P, HEAD_PAIR * E], BF16, name="sum_bank")
+            for h in range(HEAD_PAIR):
+                nc.tensor.matmul(
+                    out=spread[:, h * E : (h + 1) * E],
+                    lhsT=ones[:],
+                    rhs=bias_row[:, h * E : (h + 1) * E],
+                    start=True,
+                    stop=True,
+                )
+            nc.vector.tensor_copy(out=first_biases[:], in_=spread[:])
+
+        scaled_bias = []
+
+        def scale_bias(h):
+            scaled = consts.tile([P, E], BF16, name="scaled_bias_%d" % h)
+            nc.gpsimd.tensor_scalar(
+                out=scaled[:],
+                in0=bias[h],
+                scalar1=float(WORDS),
+                scalar2=0.0,
+                op0=ALU.mult,
+                op1=ALU.add,
+            )
+            scaled_bias.append(scaled)
 
         def turn(piece, half):
             row_words = piece["raw"][half][:].bitcast(F32)
@@ -162,7 +186,7 @@ def tile_biencodermodel_pa_kernel(tc, feature, aspect_v, W, b, out_0, out_1):
             vector = vectors.tile([P, E], F32)
             if t < WORDS:
                 nc.vector.tensor_tensor(
-                    out=vector[:], in0=product[:], in1=bias[h][:], op=ALU.add
+                    out=vector[:], in0=product[:], in1=bias[h], op=ALU.add
                 )
             else:
                 nc.vector.scalar_tensor_tensor(
@@ -197,40 +221,43 @@ def tile_biencodermodel_pa_kernel(tc, feature, aspect_v, W, b, out_0, out_1):
                 )
                 group["weight"] = weight
 
-        def make_diagonal(group, word):
-            diagonal = diagonals.tile([P, P], F32)
-            nc.scalar.activation(
-                out=diagonal[:],
-                in_=identity[:],
-                func=ACT.Copy,
-                scale=group["weight"][:, word : word + 1],
-            )
-            group["diagonals"][word] = diagonal
+        def make_diagonals(group):
+            for word in group["tensor"]:
+                diagonal = diagonals.tile([P, P], F32)
+                nc.scalar.activation(
+                    out=diagonal[:],
+                    in_=identity[:],
+                    func=ACT.Copy,
+                    scale=group["weight"][:, word : word + 1],
+                )
+                group["diagonals"][word] = diagonal
 
-        def tensor_add(group, n):
-            if n == 0:
-                tensor_sum = sum_psum.tile([P, E], F32)
-                group["sum"] = tensor_sum
-            word = group["tensor"][n]
-            nc.tensor.matmul(
-                out=group["sum"][:],
-                lhsT=group["diagonals"][word][:],
-                rhs=group["vectors"][word][:],
-                start=(n == 0),
-                stop=(n == len(group["tensor"]) - 1),
-            )
+        def tensor_sum(group):
+            bank = sum_psum.tile([P, E], F32, name="sum_bank")
+            for word in group["tensor"]:
+                nc.tensor.matmul(
+                    out=bank[:],
+                    lhsT=group["diagonals"][word][:],
+                    rhs=group["vectors"][word][:],
+                    start=(word == group["tensor"][0]),
+                    stop=(word == group["tensor"][-1]),
+                )
+            group["sum"] = bank
 
-        def vector_add(group, word):
-            total = sums.tile([P, E], F32)
-            nc.vector.scalar_tensor_tensor(
-                out=total[:],
-                in0=group["vectors"][word][:],
-                scalar=group["weight"][:, word : word + 1],
-                in1=group["sum"][:],
-                op0=ALU.mult,
-                op1=ALU.add,
-            )
-            group["sum"] = total
+        def vector_add(group, g):
+            for word in group["vector"]:
+                total = sums.tile([P, E], F32)
+                nc.vector.scalar_tensor_tensor(
+                    out=total[:],
+                    in0=group["vectors"][word][:],
+                    scalar=group["weight"][:, word : word + 1],
+                    in1=group["sum"][:],
+                    op0=ALU.mult,
+                    op1=ALU.add,
+                )
+                group["sum"] = total
+            if not group["gpsimd"]:
+                store_mean(group, g, group["sum"])
 
         def weigh_alone(group, t, step):
             if step == 0:
@@ -328,9 +355,11 @@ def tile_biencodermodel_pa_kernel(tc, feature, aspect_v, W, b, out_0, out_1):
         ]
 
         def split(g):
+            if g == GROUPS - 2:
+                return {"tensor": [1, 2, 3], "vector": [0], "gpsimd": []}
             if g >= GROUPS - LATE_GROUPS:
                 return {"tensor": [2, 3], "vector": [1, 0], "gpsimd": []}
-            if g % 3 == 0:
+            if g % 3 == 0 and g < GROUPS - EASED_GROUPS:
                 return {"tensor": [3], "vector": [1], "gpsimd": [0, 2]}
             return {"tensor": [2, 3], "vector": [1], "gpsimd": [0]}
 
@@ -345,21 +374,30 @@ def tile_biencodermodel_pa_kernel(tc, feature, aspect_v, W, b, out_0, out_1):
         interleave(words[0], 1, nc.scalar.copy)
         quantise(words[0], 0, 1)
         quantise(words[0], 1, 1)
+        spread_biases()
+        turn(senses, 0)
+        turn(senses, 1)
+        interleave(senses, 0, nc.scalar.copy)
+        interleave(senses, 1, nc.scalar.copy)
+        for h in range(HEAD_PAIR):
+            scale_bias(h)
 
         turns = [[]] + [[(piece, 0), (piece, 1)] for piece in words[2:]]
         turns += [[(piece, half)] for piece in weights[HEAD_PAIR:] for half in range(2)]
 
         groups = []
-        for g in range(GROUPS + MEAN_LAG):
-            if g < GROUPS:
-                sum_squares = norms.tile([P, TILES], F32)
-                group = {"sum_squares": sum_squares, "vectors": {}, "weights": {}, "above": {}, "diagonals": {}}
-                group.update(split(g))
-                groups.append(group)
+        for g in range(GROUPS):
+            sum_squares = norms.tile([P, TILES], F32)
+            group = {"sum_squares": sum_squares, "vectors": {}, "weights": {}, "above": {}, "diagonals": {}}
+            group.update(split(g))
+            groups.append(group)
             closing = g == GROUPS - 1
+            for h in range(HEAD_PAIR, HEADS):
+                if g == order.index((h, 0)) - BIAS_LEAD:
+                    scale_bias(h)
 
             def back(lag):
-                return groups[g - lag] if lag <= g < GROUPS - 1 + lag else None
+                return groups[g - lag] if lag <= g else None
 
             turned = turns[g] if g < len(turns) else []
             ready = [piece for piece, half in turns[g - 1] if half == 1] if 1 <= g <= len(turns) else []
@@ -368,45 +406,24 @@ def tile_biencodermodel_pa_kernel(tc, feature, aspect_v, W, b, out_0, out_1):
             for t in range(TILES):
                 if t in TURN_STEPS[: len(turned)]:
                     turn(*turned[TURN_STEPS.index(t)])
-                if t == 1 and back(SUM_LAG) is not None:
+                if back(SUM_LAG) is not None and t == SUM_STEP:
                     for word in back(SUM_LAG)["gpsimd"]:
                         gpsimd_term(back(SUM_LAG), word)
-                if t == 2 and back(SENSES_LAG) is not None:
+                    tensor_sum(back(SUM_LAG))
+                if back(SENSES_LAG) is not None and t == SENSES_STEP:
                     finish_senses(back(SENSES_LAG), g - SENSES_LAG)
-                for lag in (SUM_LAG, SUM_LAG - 1):
-                    f = g - lag
-                    if back(lag) is None or (f >= GROUPS - LATE_GROUPS) != (lag < SUM_LAG):
-                        continue
-                    steps = SUM_STEPS if lag == SUM_LAG else (TILES - 1, TILES - 1)
-                    for n in range(len(back(lag)["tensor"])):
-                        if t == steps[n]:
-                            tensor_add(back(lag), n)
-                f = g - SUM_LAG
-                if t == ADD_STEP and 0 <= f < GROUPS - LATE_GROUPS:
-                    vector_add(groups[f], 1)
-                if t == 0 and g - SUM_LAG >= GROUPS - LATE_GROUPS and back(SUM_LAG) is not None:
-                    for word in back(SUM_LAG)["vector"]:
-                        vector_add(back(SUM_LAG), word)
-                    if not back(SUM_LAG)["gpsimd"]:
-                        store_mean(back(SUM_LAG), g - SUM_LAG, back(SUM_LAG)["sum"])
-                if g == GROUPS and t == 1:
-                    finish_senses(group, g - 1)
-                    for word in range(1, WORDS):
-                        vector_sum(group, g - 1, word)
-                if g < GROUPS:
-                    project(groups[g], g, (t - 1) % TILES if closing else t)
+                if back(SUM_LAG) is not None and t == ADD_STEP:
+                    vector_add(back(SUM_LAG), g - SUM_LAG)
+                project(group, g, (t - 1) % TILES if closing else t)
                 if back(1) is not None:
                     if t < 2:
                         weigh(back(1), t)
                     if t == 3:
-                        for word in back(1)["tensor"]:
-                            make_diagonal(back(1), word)
+                        make_diagonals(back(1))
                 if closing and t >= 1:
                     weigh_alone(group, (t - 2) % TILES, 0)
                 if closing and t >= 2:
                     weigh_alone(group, (t - 3) % TILES, 1)
-                if closing and t == 4:
-                    vector_sum(group, g, 0)
                 if t in TURN_STEPS[: len(turned)]:
                     n = TURN_STEPS.index(t)
                     interleave(*turned[n], nc.scalar.copy if n == 0 else nc.vector.tensor_copy)
@@ -415,25 +432,29 @@ def tile_biencodermodel_pa_kernel(tc, feature, aspect_v, W, b, out_0, out_1):
                         quantise(piece)
                 if g == 0:
                     if t == 1:
-                        turn(senses, 0)
-                        turn(senses, 1)
-                        interleave(senses, 0, nc.scalar.copy)
-                        interleave(senses, 1, nc.scalar.copy)
-                    if t == 3:
-                        quantise(senses)
                         turn(weights[1], 0)
                         turn(weights[1], 1)
-                        interleave(weights[1], 0, nc.scalar.copy)
+                        interleave(weights[1], 0, nc.vector.tensor_copy)
                         interleave(weights[1], 1, nc.scalar.copy)
-                    if t == 4:
+                    if t == 2:
+                        quantise(senses)
                         quantise(weights[1])
                         turn(words[1], 0)
                         turn(words[1], 1)
                         interleave(words[1], 0, nc.scalar.copy)
                         interleave(words[1], 1, nc.scalar.copy)
-            if closing:
-                weigh_alone(group, WORDS - 1, 0)
-                weigh_alone(group, WORDS - 2, 1)
-                weigh_alone(group, WORDS - 1, 1)
-            if back(MEAN_LAG) is not None and back(MEAN_LAG)["gpsimd"]:
+            if back(MEAN_LAG) is not None:
                 gpsimd_add(back(MEAN_LAG), g - MEAN_LAG)
+
+        weigh_alone(group, WORDS - 1, 0)
+        weigh_alone(group, WORDS - 2, 1)
+        weigh_alone(group, WORDS - 1, 1)
+        tensor_sum(groups[-3])
+        tensor_sum(groups[-2])
+        finish_senses(groups[-2], GROUPS - 2)
+        finish_senses(group, GROUPS - 1)
+        gpsimd_add(groups[-4], GROUPS - 4)
+        vector_add(groups[-3], GROUPS - 3)
+        for word in range(WORDS):
+            vector_sum(group, GROUPS - 1, word)
+        vector_add(groups[-2], GROUPS - 2)

from contextlib import ExitStack

import concourse.mybir as mybir
from concourse.masks import make_identity

F32 = mybir.dt.float32
BF16 = mybir.dt.bfloat16
U32 = mybir.dt.uint32
U8 = mybir.dt.uint8
FP8X4 = mybir.dt.float8_e4m3fn_x4
ALU = mybir.AluOpType
ACT = mybir.ActivationFunctionType

P = 128
PACK = 4
SENSES, WORDS, K = 512, 4, 512
HEADS, E = 6, 512
EPS = 1e-12

BLOCKS = 4
PARITIES = 2
HALF = BLOCKS // 2
SENSE_BLOCKS = SENSES // P
HEAD_PAIR = 2
GROUPS = HEADS * SENSE_BLOCKS
TILES = WORDS + 1
TURN_STEPS = (2, 4)
QUANTISE_STEP = 2
SENSES_LAG = 2
SUM_LAG = 3
MEAN_LAG = 4
SUM_STEP = 1
SENSES_STEP = 2
ADD_STEP = 4
BIAS_LEAD = 6
LATE_GROUPS = 3
EASED_GROUPS = 6

FLOPS = 2 * (SENSES + SENSES * WORDS) * K * HEADS * E


def tile_biencodermodel_pa_kernel(tc, feature, aspect_v, W, b, out_0, out_1):
    nc = tc.nc
    with ExitStack() as ctx:
        consts = ctx.enter_context(tc.tile_pool(name="consts", bufs=1))
        operands = ctx.enter_context(tc.tile_pool(name="operands", bufs=1))
        staging = ctx.enter_context(tc.tile_pool(name="staging", bufs=4))
        vectors = ctx.enter_context(tc.tile_pool(name="vectors", bufs=(MEAN_LAG + 1) * TILES))
        squares = ctx.enter_context(tc.tile_pool(name="squares", bufs=2))
        norms = ctx.enter_context(tc.tile_pool(name="norms", bufs=MEAN_LAG + 2))
        column_halves = ctx.enter_context(tc.tile_pool(name="column_halves", bufs=4 * WORDS))
        diagonals = ctx.enter_context(tc.tile_pool(name="diagonals", bufs=2 * MEAN_LAG))
        sums = ctx.enter_context(tc.tile_pool(name="sums", bufs=8))
        results = ctx.enter_context(tc.tile_pool(name="results", bufs=3))
        sum_psum = ctx.enter_context(tc.psum_pool(name="sum_psum", bufs=2))
        main_psum = ctx.enter_context(tc.psum_pool(name="main_psum", bufs=6))
        ctx.enter_context(tc.manual_schedule())

        def load_piece(rows, name):
            raw = []
            for half in range(2):
                raw_half = operands.tile([P, HALF * K], BF16, name="raw_%s_%d" % (name, half))
                nc.sync.dma_start(
                    out=raw_half[:].rearrange("p (c k) -> p c k", c=HALF),
                    in_=rows[:, half * HALF : (half + 1) * HALF],
                )
                raw.append(raw_half)
            codes = operands.tile([P, BLOCKS * P], U32, name="codes_" + name, align_bytes=64)
            scales = operands.tile([P, BLOCKS * P], U8, name="scales_" + name, align_bytes=64)
            return {"raw": raw, "codes": codes, "scales": scales}

        def load_weights(h):
            return load_piece(W[h].rearrange("(c p) k -> p c k", p=P), "w%d" % h)

        def load_words(i):
            return load_piece(feature[i * P : (i + 1) * P], "f%d" % i)

        loaded_row = consts.tile([P, HEAD_PAIR * E], BF16)
        nc.sync.dma_start(
            out=loaded_row[0:1, :], in_=b[0:HEAD_PAIR].rearrange("(o h) e -> o (h e)", o=1)
        )
        bias_row = consts.tile([P, HEAD_PAIR * E], BF16)
        nc.vector.memset(bias_row[:].bitcast(F32), 0.0)
        ones = consts.tile([P, P], BF16)
        nc.vector.memset(ones[:], 1.0)

        weights = [load_weights(0)]
        words = [load_words(0)]
        senses = load_piece(aspect_v.rearrange("(c p) k -> p c k", p=P), "a")
        weights.append(load_weights(1))
        words += [load_words(i) for i in range(1, SENSE_BLOCKS)]
        weights += [load_weights(h) for h in range(HEAD_PAIR, HEADS)]
        first_biases = consts.tile([P, HEAD_PAIR * E], BF16)
        bias = [first_biases[:, h * E : (h + 1) * E] for h in range(HEAD_PAIR)]
        for h in range(HEAD_PAIR, HEADS):
            head_bias = consts.tile([P, E], BF16, name="bias_%d" % h)
            nc.sync.dma_start(out=head_bias[:], in_=b[h].partition_broadcast(P))
            bias.append(head_bias[:])

        identity = consts.tile([P, P], F32)
        make_identity(nc, identity[:])
        floor = consts.tile([P, 1], F32)
        nc.vector.memset(floor[:], (WORDS * EPS) ** 2)
        minus_floor = consts.tile([P, 1], F32)
        nc.vector.memset(minus_floor[:], -((WORDS * EPS) ** 2))
        warm = consts.tile([P, 1], F32)
        nc.vector.memset(warm[:], 1.0)
        warmed = consts.tile([P, 1], F32)
        nc.scalar.activation(out=warmed[:], in_=warm[:], func=ACT.Abs_reciprocal_sqrt)

        nc.vector.tensor_copy(out=bias_row[0:1, :], in_=loaded_row[0:1, :])

        def spread_biases():
            spread = sum_psum.tile([P, HEAD_PAIR * E], BF16, name="sum_bank")
            for h in range(HEAD_PAIR):
                nc.tensor.matmul(
                    out=spread[:, h * E : (h + 1) * E],
                    lhsT=ones[:],
                    rhs=bias_row[:, h * E : (h + 1) * E],
                    start=True,
                    stop=True,
                )
            nc.vector.tensor_copy(out=first_biases[:], in_=spread[:])

        scaled_bias = []

        def scale_bias(h):
            scaled = consts.tile([P, E], BF16, name="scaled_bias_%d" % h)
            nc.gpsimd.tensor_scalar(
                out=scaled[:],
                in0=bias[h],
                scalar1=float(WORDS),
                scalar2=0.0,
                op0=ALU.mult,
                op1=ALU.add,
            )
            scaled_bias.append(scaled)

        def turn(piece, half):
            row_words = piece["raw"][half][:].bitcast(F32)
            turned = main_psum.tile([P, HALF, PARITIES, P], F32, name="bank")
            for c in range(HALF):
                for u in range(PARITIES):
                    first = c * PARITIES * P
                    nc.tensor.transpose(
                        turned[:, c, u, :],
                        row_words[:, first + u : first + PARITIES * P : PARITIES],
                        identity[:],
                    )
            piece["turned"] = piece.get("turned", []) + [turned]

        def interleave(piece, half, copy):
            if "grouped" not in piece:
                grouped = staging.tile([P, BLOCKS * P * PACK], BF16, align_bytes=64)
                piece["grouped"] = grouped
            width = HALF * P * PACK
            copy(
                out=piece["grouped"][:, half * width : (half + 1) * width]
                .bitcast(F32)
                .rearrange("p (c r u) -> p c r u", c=HALF, u=PARITIES),
                in_=piece["turned"][half][:].rearrange("p c u r -> p c r u"),
            )

        def quantise(piece, first_half=0, halves=2):
            first, last = first_half * HALF * P, (first_half + halves) * HALF * P
            nc.vector.quantize_mx(
                out=piece["codes"][:, first:last].bitcast(FP8X4),
                scales=piece["scales"][:, first:last],
                in_=piece["grouped"][:, first * PACK : last * PACK],
            )

        def project(group, g, t):
            h, i = order[g]
            rows, block = (words[i], t) if t < WORDS else (senses, i)
            cols = slice(block * P, (block + 1) * P)
            product = main_psum.tile([P, E], F32, name="bank")
            nc.tensor.matmul_mx(
                out=product[:],
                lhsT=rows["codes"][:, cols].bitcast(FP8X4),
                lhsT_scale=rows["scales"][:, cols],
                rhs=weights[h]["codes"][:].bitcast(FP8X4),
                rhs_scale=weights[h]["scales"][:],
                start=True,
                stop=True,
            )
            vector = vectors.tile([P, E], F32)
            if t < WORDS:
                nc.vector.tensor_tensor(
                    out=vector[:], in0=product[:], in1=bias[h], op=ALU.add
                )
            else:
                nc.vector.scalar_tensor_tensor(
                    out=vector[:],
                    in0=product[:],
                    scalar=float(WORDS),
                    in1=scaled_bias[h][:],
                    op0=ALU.mult,
                    op1=ALU.add,
                )
            unread = squares.tile([P, E], F32)
            nc.scalar.activation(
                out=unread[:],
                in_=vector[:],
                func=ACT.Square,
                scale=float(WORDS) if t < WORDS else 1.0,
                accum_out=group["sum_squares"][:, t : t + 1],
            )
            group["vectors"][t] = vector

        def weigh(group, step):
            if step == 0:
                above = norms.tile([P, TILES], F32)
                nc.scalar.activation(
                    out=above[:], in_=group["sum_squares"][:], func=ACT.Relu, bias=minus_floor[:]
                )
                group["above"] = above
            else:
                weight = norms.tile([P, TILES], F32)
                nc.scalar.activation(
                    out=weight[:], in_=group["above"][:], func=ACT.Abs_reciprocal_sqrt, bias=floor[:]
                )
                group["weight"] = weight

        def make_diagonals(group):
            for word in group["tensor"]:
                diagonal = diagonals.tile([P, P], F32)
                nc.scalar.activation(
                    out=diagonal[:],
                    in_=identity[:],
                    func=ACT.Copy,
                    scale=group["weight"][:, word : word + 1],
                )
                group["diagonals"][word] = diagonal

        def tensor_sum(group):
            bank = sum_psum.tile([P, E], F32, name="sum_bank")
            for word in group["tensor"]:
                nc.tensor.matmul(
                    out=bank[:],
                    lhsT=group["diagonals"][word][:],
                    rhs=group["vectors"][word][:],
                    start=(word == group["tensor"][0]),
                    stop=(word == group["tensor"][-1]),
                )
            group["sum"] = bank

        def vector_add(group, g):
            for word in group["vector"]:
                total = sums.tile([P, E], F32)
                nc.vector.scalar_tensor_tensor(
                    out=total[:],
                    in0=group["vectors"][word][:],
                    scalar=group["weight"][:, word : word + 1],
                    in1=group["sum"][:],
                    op0=ALU.mult,
                    op1=ALU.add,
                )
                group["sum"] = total
            if not group["gpsimd"]:
                store_mean(group, g, group["sum"])

        def weigh_alone(group, t, step):
            if step == 0:
                above = norms.tile([P, 1], F32, name="above_alone")
                nc.scalar.activation(
                    out=above[:], in_=group["sum_squares"][:, t : t + 1], func=ACT.Relu, bias=minus_floor[:]
                )
                group["above"][t] = above
            else:
                weight = norms.tile([P, 1], F32, name="weight_alone")
                nc.scalar.activation(
                    out=weight[:], in_=group["above"][t][:], func=ACT.Abs_reciprocal_sqrt, bias=floor[:]
                )
                group["weights"][t] = weight

        def vector_sum(group, g, word):
            h, i = order[g]
            totals = []
            for half in range(2):
                cols = slice(half * E // 2, (half + 1) * E // 2)
                total = column_halves.tile([P, E // 2], F32)
                if word == 0:
                    nc.vector.tensor_scalar(
                        out=total[:],
                        in0=group["vectors"][word][:, cols],
                        scalar1=group["weights"][word][:],
                        scalar2=None,
                        op0=ALU.mult,
                    )
                else:
                    nc.vector.scalar_tensor_tensor(
                        out=total[:],
                        in0=group["vectors"][word][:, cols],
                        scalar=group["weights"][word][:],
                        in1=group["totals"][half][:],
                        op0=ALU.mult,
                        op1=ALU.add,
                    )
                if word == WORDS - 1:
                    nc.sync.dma_start(out=out_1[h, i * P : (i + 1) * P, cols], in_=total[:])
                totals.append(total)
            group["totals"] = totals

        def gpsimd_term(group, word):
            term = results.tile([P, E], F32)
            nc.gpsimd.tensor_scalar(
                out=term[:],
                in0=group["vectors"][word][:],
                scalar1=group["weight"][:, word : word + 1],
                scalar2=0.0,
                op0=ALU.mult,
                op1=ALU.add,
            )
            if "term" in group:
                terms = results.tile([P, E], F32)
                nc.gpsimd.tensor_tensor(out=terms[:], in0=group["term"][:], in1=term[:], op=ALU.add)
                group["term"] = terms
            else:
                group["term"] = term

        def gpsimd_add(group, g):
            mean = results.tile([P, E], F32)
            nc.gpsimd.tensor_tensor(
                out=mean[:], in0=group["term"][:], in1=group["sum"][:], op=ALU.add
            )
            store_mean(group, g, mean)

        def store_mean(group, g, mean):
            h, i = order[g]
            nc.sync.dma_start(out=out_1[h, i * P : (i + 1) * P, :], in_=mean[:])

        def finish_senses(group, g):
            h, i = order[g]
            unit = results.tile([P, E], F32)
            if g == GROUPS - 1:
                nc.scalar.activation(
                    out=unit[:], in_=group["vectors"][WORDS][:], func=ACT.Copy, scale=group["weights"][WORDS][:]
                )
            else:
                nc.gpsimd.tensor_scalar(
                    out=unit[:],
                    in0=group["vectors"][WORDS][:],
                    scalar1=group["weight"][:, WORDS : WORDS + 1],
                    scalar2=0.0,
                    op0=ALU.mult,
                    op1=ALU.add,
                )
            nc.sync.dma_start(out=out_0[h, i * P : (i + 1) * P, :], in_=unit[:])

        order = [
            (h, i)
            for first in range(0, HEADS, HEAD_PAIR)
            for i in range(SENSE_BLOCKS)
            for h in range(first, first + HEAD_PAIR)
        ]

        def split(g):
            if g == GROUPS - 2:
                return {"tensor": [1, 2, 3], "vector": [0], "gpsimd": []}
            if g >= GROUPS - LATE_GROUPS:
                return {"tensor": [2, 3], "vector": [1, 0], "gpsimd": []}
            if g % 3 == 0 and g < GROUPS - EASED_GROUPS:
                return {"tensor": [3], "vector": [1], "gpsimd": [0, 2]}
            return {"tensor": [2, 3], "vector": [1], "gpsimd": [0]}

        turn(weights[0], 0)
        turn(weights[0], 1)
        interleave(weights[0], 0, nc.scalar.copy)
        interleave(weights[0], 1, nc.vector.tensor_copy)
        quantise(weights[0])
        turn(words[0], 0)
        turn(words[0], 1)
        interleave(words[0], 0, nc.scalar.copy)
        interleave(words[0], 1, nc.scalar.copy)
        quantise(words[0], 0, 1)
        quantise(words[0], 1, 1)
        spread_biases()
        turn(senses, 0)
        turn(senses, 1)
        interleave(senses, 0, nc.scalar.copy)
        interleave(senses, 1, nc.scalar.copy)
        for h in range(HEAD_PAIR):
            scale_bias(h)

        turns = [[]] + [[(piece, 0), (piece, 1)] for piece in words[2:]]
        turns += [[(piece, half)] for piece in weights[HEAD_PAIR:] for half in range(2)]

        groups = []
        for g in range(GROUPS):
            sum_squares = norms.tile([P, TILES], F32)
            group = {"sum_squares": sum_squares, "vectors": {}, "weights": {}, "above": {}, "diagonals": {}}
            group.update(split(g))
            groups.append(group)
            closing = g == GROUPS - 1
            for h in range(HEAD_PAIR, HEADS):
                if g == order.index((h, 0)) - BIAS_LEAD:
                    scale_bias(h)

            def back(lag):
                return groups[g - lag] if lag <= g else None

            turned = turns[g] if g < len(turns) else []
            ready = [piece for piece, half in turns[g - 1] if half == 1] if 1 <= g <= len(turns) else []
            if g == 1:
                ready = [words[1]]
            for t in range(TILES):
                if t in TURN_STEPS[: len(turned)]:
                    turn(*turned[TURN_STEPS.index(t)])
                if back(SUM_LAG) is not None and t == SUM_STEP:
                    for word in back(SUM_LAG)["gpsimd"]:
                        gpsimd_term(back(SUM_LAG), word)
                    tensor_sum(back(SUM_LAG))
                if back(SENSES_LAG) is not None and t == SENSES_STEP:
                    finish_senses(back(SENSES_LAG), g - SENSES_LAG)
                if back(SUM_LAG) is not None and t == ADD_STEP:
                    vector_add(back(SUM_LAG), g - SUM_LAG)
                project(group, g, (t - 1) % TILES if closing else t)
                if back(1) is not None:
                    if t < 2:
                        weigh(back(1), t)
                    if t == 3:
                        make_diagonals(back(1))
                if closing and t >= 1:
                    weigh_alone(group, (t - 2) % TILES, 0)
                if closing and t >= 2:
                    weigh_alone(group, (t - 3) % TILES, 1)
                if t in TURN_STEPS[: len(turned)]:
                    n = TURN_STEPS.index(t)
                    interleave(*turned[n], nc.scalar.copy if n == 0 else nc.vector.tensor_copy)
                if t == QUANTISE_STEP:
                    for piece in ready:
                        quantise(piece)
                if g == 0:
                    if t == 1:
                        turn(weights[1], 0)
                        turn(weights[1], 1)
                        interleave(weights[1], 0, nc.vector.tensor_copy)
                        interleave(weights[1], 1, nc.scalar.copy)
                    if t == 2:
                        quantise(senses)
                        quantise(weights[1])
                        turn(words[1], 0)
                        turn(words[1], 1)
                        interleave(words[1], 0, nc.scalar.copy)
                        interleave(words[1], 1, nc.scalar.copy)
            if back(MEAN_LAG) is not None:
                gpsimd_add(back(MEAN_LAG), g - MEAN_LAG)

        weigh_alone(group, WORDS - 1, 0)
        weigh_alone(group, WORDS - 2, 1)
        weigh_alone(group, WORDS - 1, 1)
        tensor_sum(groups[-3])
        tensor_sum(groups[-2])
        finish_senses(groups[-2], GROUPS - 2)
        finish_senses(group, GROUPS - 1)
        gpsimd_add(groups[-4], GROUPS - 4)
        vector_add(groups[-3], GROUPS - 3)
        for word in range(WORDS):
            vector_sum(group, GROUPS - 1, word)
        vector_add(groups[-2], GROUPS - 2)
